import numpy as np
import ml_dtypes


def mxq(x, axis, fmt="e4m3"):
    dtype, down = {"e4m3": (ml_dtypes.float8_e4m3fn, 7), "e5m2": (ml_dtypes.float8_e5m2, 14)}[fmt]
    v = np.moveaxis(np.asarray(x, np.float32).astype(ml_dtypes.bfloat16).astype(np.float64), axis, -1)
    blocks = v.reshape(v.shape[:-1] + (-1, 32))
    amax = np.abs(blocks).max(-1, keepdims=True)
    byte = np.maximum(np.where(amax > 0, np.frexp(amax)[1] - 1 + 127, 0) - down, 1)
    scale = np.exp2(byte - 127.0)
    codes = (blocks / scale).astype(np.float32).astype(dtype).astype(np.float64)
    return np.moveaxis((codes * scale).reshape(v.shape), -1, axis)


WIDE = False


def mx_kscale(k):
    if not WIDE:
        return np.ones(k)
    levels = np.array([18, -18])
    if k % 512:
        return np.exp2(np.random.permutation(np.resize(levels, k // 32))).repeat(32)
    a = np.empty((k // 512, 16))
    for p in range(k // 512):
        a[p, :8] = np.random.permutation(np.resize(levels, 8))
        for g in range(8):
            far = levels[np.abs(levels - a[p, g]) >= 10]
            a[p, g + 8] = far[np.random.randint(len(far))]
    return np.exp2(a.ravel()).repeat(32)


BF16 = ml_dtypes.bfloat16


def bf(x):
    return np.asarray(x, np.float32).astype(BF16)


def f64(x):
    return np.asarray(x).astype(np.float64)


B, N, DIM, H, DK, DV = 1, 1024, 1024, 16, 16, 64
WT = 256.0
EPS = 1e-12
DI = H * (DK + DV)


def heads(t):
    return f64(t).reshape(B, N, H, DK + DV).transpose(0, 2, 1, 3)


def flat(t):
    return t.transpose(0, 2, 1, 3).reshape(B * N, -1)


def rot_table(sm_log):
    w = np.exp(f64(sm_log)) + 1.0
    gamma = np.where(w < WT, 0.5 * (np.cos(np.pi * w / WT) + 1.0), 0.0)
    freq = np.pi * gamma / w
    ang = freq[:, None] * np.arange(N, dtype=np.float64)[None, :]
    return np.stack([np.cos(ang), np.sin(ang)])


def norm_back(t, d):
    r = 1.0 / np.maximum(np.sqrt((t * t).sum(-1, keepdims=True)), EPS)
    tn = t * r
    return r * (d - tn * (d * tn).sum(-1, keepdims=True))


def setup_inputs():
    s = mx_kscale(N)
    uqk = mx_kscale(2 * H * DK)
    ug = mx_kscale(H * DV)
    uv = np.repeat(mx_kscale(H * DV // 2), 2)
    uq, uk = uqk[:H * DK].reshape(H, DK), uqk[H * DK:].reshape(H, DK)
    ug, uv = ug.reshape(H, DV), uv.reshape(H, DV)
    u_qg = np.concatenate([uq, ug], axis=1).reshape(DI, 1)
    u_kv = np.concatenate([uk, uv], axis=1).reshape(DI, 1)
    x0 = bf(np.random.standard_normal((B, N, DIM)))
    wqg0 = bf(np.random.standard_normal((DI, DIM)) / np.sqrt(DIM))
    wkv0 = bf(np.random.standard_normal((DI, DIM)) / np.sqrt(DIM))
    sm_log = bf(np.linspace(3.0, 5.8, H) + 0.1 * np.random.standard_normal(H))
    qg = f64(x0) @ f64(wqg0).T
    kv = f64(x0) @ f64(wkv0).T
    rot = rot_table(sm_log)

    def grad(d, scale, u):
        e = np.exp2(np.random.randint(-6, 1, (B, 1, N, 1)))
        return bf(np.random.standard_normal((B, H, N, d)) * e * scale / s[None, None, :, None] * u[None, :, None, :])

    g0 = grad(DK, 4.0, uq)
    g1 = grad(DV, 1.0, ug)
    g2 = grad(DK, 4.0, uk)
    g3 = grad(DV, 8.0, uv)
    return {'tokens': bf(f64(x0) * s[None, :, None]),
            'w_qg': bf(f64(wqg0) / u_qg),
            'w_kv': bf(f64(wkv0) / u_kv),
            'sm_log': sm_log,
            'qg': np.asarray(qg, np.float32),
            'kv': np.asarray(kv, np.float32),
            'rot': np.asarray(rot, np.float32),
            'grad_0': g0, 'grad_1': g1, 'grad_2': g2, 'grad_3': g3}


def reference(tokens, w_qg, w_kv, sm_log, qg, kv, rot, grad_0, grad_1, grad_2, grad_3):
    a, c = heads(qg), heads(kv)
    q, g = a[..., :DK], a[..., DK:]
    k, v = c[..., :DK], c[..., DK:]
    tab = f64(rot)
    cos = tab[0][None, :, :, None]
    sin = tab[1][None, :, :, None]

    def rotate_back(d):
        d0, d1 = d[..., 0:1], d[..., 1:2]
        return np.concatenate([d0 * cos + d1 * sin, d1 * cos - d0 * sin, d[..., 2:]], axis=-1)

    dq = norm_back(q, rotate_back(f64(grad_0)))
    dk = norm_back(k, rotate_back(f64(grad_2)))
    dv = norm_back(v, f64(grad_3))
    sg = 1.0 / (1.0 + np.exp(-g))
    th = np.tanh(g * sg)
    dg = f64(grad_1) * (1.0 - th * th) * (sg * (1.0 + g * (1.0 - sg)))
    dz = np.concatenate([flat(dq), flat(dk), flat(dg), flat(dv)], axis=1)
    wa = f64(w_qg).reshape(H, DK + DV, DIM)
    wc = f64(w_kv).reshape(H, DK + DV, DIM)
    wj = np.concatenate([wa[:, :DK].reshape(H * DK, DIM), wc[:, :DK].reshape(H * DK, DIM),
                         wa[:, DK:].reshape(H * DV, DIM), wc[:, DK:].reshape(H * DV, DIM)], axis=0)
    dx = (mxq(dz, 1, 'e5m2') @ mxq(wj, 0, 'e4m3')).reshape(B, N, DIM)
    xt = mxq(f64(tokens).reshape(B * N, DIM), 0, 'e4m3')
    dw = mxq(dz, 0, 'e5m2').T @ xt
    i1, i2, i3 = H * DK, 2 * H * DK, 2 * H * DK + H * DV
    dw_q = dw[:i1].reshape(H, DK, DIM)
    dw_k = dw[i1:i2].reshape(H, DK, DIM)
    dw_g = dw[i2:i3].reshape(H, DV, DIM)
    dw_v = dw[i3:].reshape(H, DV, DIM)
    dw_qg = np.concatenate([dw_q, dw_g], axis=1).reshape(DI, DIM)
    dw_kv = np.concatenate([dw_k, dw_v], axis=1).reshape(DI, DIM)
    return dx, dw_qg, dw_kv

@@ -1,0 +1,513 @@
+from contextlib import ExitStack
+
+import concourse.mybir as mybir
+from concourse.masks import make_identity
+
+N, DIM, H, DK, DV = 1024, 1024, 16, 16, 64
+HD = DK + DV
+DI = H * HD
+FLOPS = 2 * 2 * N * (2 * DI) * DIM
+
+F32 = mybir.dt.float32
+BF16 = mybir.dt.bfloat16
+U32 = mybir.dt.uint32
+U8 = mybir.dt.uint8
+I32 = mybir.dt.int32
+E4M3 = mybir.dt.float8_e4m3fn_x4
+E5M2 = mybir.dt.float8_e5m2_x4
+AF = mybir.ActivationFunctionType
+ALU = mybir.AluOpType
+AX = mybir.AxisListType
+
+P = 128
+J = 4
+GT = 512
+HH = 8
+HALF = HH * HD
+
+
+def tile_gatedscreeningtile_pa_v_kernel(
+    tc, tokens, w_qg, w_kv, sm_log, qg, kv, rot, grad_0, grad_1, grad_2, grad_3, out_0, out_1, out_2
+):
+    nc = tc.nc
+    with ExitStack() as ctx:
+        const = ctx.enter_context(tc.tile_pool(name="const", bufs=1))
+        ld = ctx.enter_context(tc.tile_pool(name="ld", bufs=5))
+        gr = ctx.enter_context(tc.tile_pool(name="gr", bufs=5))
+        tmp = ctx.enter_context(tc.tile_pool(name="tmp", bufs=9))
+        dzp = ctx.enter_context(tc.tile_pool(name="dzp", bufs=3))
+        ilp = ctx.enter_context(tc.tile_pool(name="ilp", bufs=2))
+        grp = ctx.enter_context(tc.tile_pool(name="grp", bufs=3))
+        keep = ctx.enter_context(tc.tile_pool(name="keep", bufs=1))
+        dztp = ctx.enter_context(tc.tile_pool(name="dztp", bufs=7))
+        small = ctx.enter_context(tc.tile_pool(name="small", bufs=2))
+        outp = ctx.enter_context(tc.tile_pool(name="outp", bufs=3))
+        ptp = ctx.enter_context(tc.psum_pool(name="ptp", bufs=3))
+        pacc = ctx.enter_context(tc.psum_pool(name="pacc", bufs=5))
+
+        warm = const.tile([P, 1], F32, name="warm")
+        nc.vector.memset(warm[:], 0.0)
+        nc.scalar.activation(out=warm[:], in_=warm[:], func=AF.Silu)
+        ident = const.tile([P, P], F32, name="ident")
+        make_identity(nc, ident[:])
+        ident_b = const.tile([P, P], BF16, name="ident_b")
+        make_identity(nc, ident_b[:])
+
+        t_codes, t_scales, w_codes, w_scales = [], [], [], []
+        for g in range(2):
+            t_codes.append(keep.tile([P, DIM], U32, name="t_codes%d" % g, align_bytes=64))
+            t_scales.append(keep.tile([P, DIM], U8, name="t_scales%d" % g, align_bytes=64))
+        for c in range(5):
+            w_codes.append(keep.tile([P, DIM], U32, name="w_codes%d" % c, align_bytes=64))
+            w_scales.append(keep.tile([P, DIM], U8, name="w_scales%d" % c, align_bytes=64))
+
+        def interleave_quantise(raw, codes, scales, on_tensor):
+            for n in range(2):
+                cols = slice(512 * n, 512 * (n + 1))
+                grouped = grp.tile([P, 512, J], BF16, name="grouped", tag="grp", align_bytes=64)
+                if on_tensor:
+                    for k in range(2):
+                        mv = ptp.tile([P, 256, J], BF16, name="mv", tag="tp")
+                        for a in range(2):
+                            c0 = 512 * n + 256 * k + 128 * a
+                            nc.tensor.matmul(
+                                mv[:, 128 * a : 128 * (a + 1), :].rearrange("p w j -> p (w j)"),
+                                lhsT=ident_b[:],
+                                rhs=raw[:, :, c0 : c0 + 128].rearrange("p j w -> p w j"),
+                                start=True,
+                                stop=True,
+                            )
+                        nc.scalar.copy(out=grouped[:, 256 * k : 256 * (k + 1), :], in_=mv[:])
+                else:
+                    nc.vector.tensor_copy(out=grouped[:], in_=raw[:, :, cols].rearrange("p j w -> p w j"))
+                nc.vector.quantize_mx(
+                    out=codes[:, cols].bitcast(E4M3),
+                    scales=scales[:, cols],
+                    in_=grouped[:].rearrange("p w j -> p (w j)"),
+                )
+
+        def prep_tokens(g):
+            raw = ld.tile([P, J, DIM], BF16, name="raw_t", tag="ld")
+            nc.sync.dma_start(
+                out=raw[:], in_=tokens[0, GT * g : GT * (g + 1), :].rearrange("(p j) w -> p j w", j=J)
+            )
+            interleave_quantise(raw, t_codes[g], t_scales[g], g == 1)
+
+        def prep_weights(c):
+            raw = ld.tile([P, J, DIM], BF16, name="raw_w", tag="ld")
+            flat = raw[:].rearrange("p j w -> p (j w)")
+            if c == 0:
+                for s, w in ((0, w_qg), (1, w_kv)):
+                    heads = w.rearrange("(h e) w -> h e w", e=HD)
+                    for pp in range(4):
+                        nc.sync.dma_start(
+                            out=flat[64 * s + pp : 64 * s + 64 : 4, :],
+                            in_=heads[:, 4 * pp : 4 * pp + 4, :].rearrange("h j w -> h (j w)"),
+                        )
+            else:
+                w = w_qg if c < 3 else w_kv
+                h0 = HH * ((c - 1) % 2)
+                for hh in range(HH):
+                    r0 = HD * (h0 + hh) + DK
+                    nc.sync.dma_start(
+                        out=flat[16 * hh : 16 * hh + 16, :],
+                        in_=w[r0 : r0 + DV, :].rearrange("(p j) w -> p (j w)", j=J),
+                    )
+            interleave_quantise(raw, w_codes[c], w_scales[c], True)
+
+        cs = const.tile([P, 2, 2, H, J], F32, name="cs")
+
+        def prep_rot():
+            rt = const.tile([P, GT], F32, name="rt")
+            nc.vector.memset(rt[64:128, :], 0.0)
+            nc.sync.dma_start(out=rt[0:64, :], in_=rot.rearrange("c h (g n) -> (c h g) n", g=2))
+            rp = ptp.tile([P, J, P], F32, name="rp", tag="tp")
+            for j in range(J):
+                nc.tensor.transpose(rp[:, j, :], rt[:, j::J], ident[:])
+            for c in range(2):
+                for g in range(2):
+                    nc.scalar.copy(
+                        out=cs[:, c, g, :, :],
+                        in_=rp[:, :, 32 * c : 32 * c + 32].rearrange("p j (h g) -> p g h j", g=2)[:, g, :, :],
+                    )
+
+        def load_half(src, g, hf):
+            t = ld.tile([P, J, HALF], F32, name="saved", tag="ld")
+            rows = src[0, GT * g : GT * (g + 1), :].rearrange("(p j) w -> p j w", j=J)
+            for lo in range(0, HALF, HALF // 2):
+                nc.sync.dma_start(
+                    out=t[:, :, lo : lo + HALF // 2], in_=rows[:, :, HALF * hf + lo : HALF * hf + lo + HALF // 2]
+                )
+            return t
+
+        def load_grad(src, g, hf):
+            t = gr.tile([P, HH, J, DV], BF16, name="grad", tag="gr")
+            nc.sync.dma_start(
+                out=t[:].rearrange("p h j f -> p h (j f)"),
+                in_=src[0, HH * hf : HH * (hf + 1), GT * g : GT * (g + 1), :].rearrange("h (p j) f -> p h (j f)", j=J),
+            )
+            return t
+
+        def load_qk_grads(g):
+            t = gr.tile([P, 2, H, J, DK], BF16, name="qkgrad", tag="gr")
+            for s, src in ((0, grad_0), (1, grad_2)):
+                nc.sync.dma_start(
+                    out=t[:, s].rearrange("p h j f -> p h (j f)"),
+                    in_=src[0, :, GT * g : GT * (g + 1), :].rearrange("h (p j) f -> p h (j f)", j=J),
+                )
+            return t
+
+        dzt = {}
+        dzc = {}
+
+        def transpose_quantise(g, c, dz, bs=(0, 1)):
+            if (g, c) not in dzt:
+                codes = dztp.tile([P, GT], U32, name="dzt_codes", tag="dztc", align_bytes=64)
+                scales = dztp.tile([P, GT], U8, name="dzt_scales", tag="dzts", align_bytes=64)
+                dzt[(g, c)] = (codes, scales)
+            codes, scales = dzt[(g, c)]
+            grouped = grp.tile([P, GT, J], BF16, name="groupedt", tag="grp", align_bytes=64)
+            gw = grouped[:].rearrange("p n t -> p (n t)").bitcast(F32)
+            for b in bs:
+                tp = ptp.tile([P, 2, 2, P], F32, name="tp", tag="tp")
+                for jj in range(2):
+                    words = dz[:, 2 * b + jj, :].bitcast(F32)
+                    for u in range(2):
+                        nc.tensor.transpose(tp[:, jj, u, :], words[:, u::2], ident[:])
+                nc.scalar.copy(
+                    out=gw[:, 512 * b : 512 * (b + 1)].rearrange("p (j r u) -> p j r u", j=2, u=2),
+                    in_=tp[:].rearrange("p j u r -> p j r u"),
+                )
+            cols = slice(256 * bs[0], 256 * (bs[-1] + 1))
+            nc.vector.quantize_mx(
+                out=codes[:, cols].bitcast(E5M2),
+                scales=scales[:, cols],
+                in_=grouped[:, cols, :].rearrange("p n t -> p (n t)"),
+            )
+
+        def bcast(ap, n):
+            return ap.rearrange("p (j h o) -> p j h o", h=HH, o=1).to_broadcast([P, J, HH, n])
+
+        def norm_factors(ss, s, n):
+            x = small.tile([P, n], F32, name="nx")
+            nc.vector.tensor_scalar(out=x[:], in0=ss[:], scalar1=1e-24, scalar2=None, op0=ALU.max)
+            y = small.tile([P, n], F32, name="ny")
+            yi = y[:].bitcast(I32)
+            nc.vector.tensor_scalar(
+                out=yi, in0=x[:].bitcast(I32), scalar1=1, scalar2=None, op0=ALU.arith_shift_right
+            )
+            nc.vector.tensor_scalar(
+                out=yi, in0=yi, scalar1=-1.0, scalar2=1597463007.0, op0=ALU.mult, op1=ALU.add
+            )
+            z = small.tile([P, n], F32, name="nz")
+            for it in range(3):
+                nc.vector.tensor_tensor(out=z[:], in0=y[:], in1=y[:], op=ALU.mult)
+                nc.vector.scalar_tensor_tensor(
+                    out=z[:], in0=z[:], scalar=-0.5, in1=x[:], op0=ALU.mult, op1=ALU.mult
+                )
+                nc.vector.scalar_tensor_tensor(
+                    out=y[:], in0=z[:], scalar=1.5, in1=y[:], op0=ALU.add, op1=ALU.mult
+                )
+            c = small.tile([P, n], F32, name="nc_")
+            nc.gpsimd.tensor_tensor(out=z[:], in0=y[:], in1=y[:], op=ALU.mult)
+            nc.gpsimd.tensor_tensor(out=c[:], in0=y[:], in1=s[:], op=ALU.mult)
+            nc.gpsimd.tensor_tensor(out=c[:], in0=c[:], in1=z[:], op=ALU.mult)
+            return y, c
+
+        def gate_scalar(a, b):
+            js = slice(2 * b, 2 * b + 2)
+            gv = a[:].rearrange("p j (h e) -> p h j e", e=HD)[:, :, js, DK:HD]
+            hh = tmp.tile([P, HH, 2, DV], F32, name="gh", tag="t")
+            nc.scalar.activation(out=hh[:], in_=gv, func=AF.Tanh, scale=0.5)
+            u = tmp.tile([P, HH, 2, DV], F32, name="gu", tag="t")
+            nc.scalar.activation(out=u[:], in_=gv, func=AF.Silu)
+            th = tmp.tile([P, HH, 2, DV], F32, name="gth", tag="t")
+            nc.scalar.activation(out=th[:], in_=u[:], func=AF.Tanh)
+            nc.scalar.activation(out=u[:], in_=u[:], func=AF.Copy, scale=0.5, bias=-0.5)
+            nc.scalar.activation(out=th[:], in_=th[:], func=AF.Square)
+            return hh, u, th
+
+        def gate_vector(st, d, b, dz):
+            hh, u, th = st
+            nc.vector.scalar_tensor_tensor(
+                out=u[:], in0=hh[:], scalar=1.0, in1=u[:], op0=ALU.subtract, op1=ALU.mult
+            )
+            nc.vector.scalar_tensor_tensor(
+                out=u[:], in0=u[:], scalar=1.0, in1=d[:, :, 2 * b : 2 * b + 2, :], op0=ALU.subtract, op1=ALU.mult
+            )
+            for jj in range(2):
+                nc.vector.scalar_tensor_tensor(
+                    out=dz[:, 2 * b + jj, :].rearrange("p (h f) -> p h f", f=DV),
+                    in0=th[:, :, jj, :],
+                    scalar=1.0,
+                    in1=u[:, :, jj, :],
+                    op0=ALU.subtract,
+                    op1=ALU.mult,
+                )
+
+        def value_sums(cc, d, ss, s):
+            tv = cc[:].rearrange("p j (h e) -> p j h e", e=HD)
+            dv = d[:].rearrange("p h j f -> p j h f")
+            junk = tmp.tile([P, J * HH, DV], BF16, name="junk", tag="t")
+            for j in range(J):
+                for h in range(HH):
+                    i = HH * j + h
+                    nc.scalar.activation(
+                        out=junk[:, i, :], in_=tv[:, j, h, DK:HD], func=AF.Square, accum_out=ss[:, 64 + i : 65 + i]
+                    )
+            for q in range(2):
+                js = slice(2 * q, 2 * q + 2)
+                pr = tmp.tile([P, 2, HH, DV], F32, name="pv", tag="t")
+                nc.vector.tensor_tensor(out=pr[:], in0=tv[:, js, :, DK:HD], in1=dv[:, js], op=ALU.mult)
+                nc.vector.tensor_reduce(
+                    out=s[:, 64 + 16 * q : 80 + 16 * q],
+                    in_=pr[:].rearrange("p j h f -> p (j h) f"),
+                    axis=AX.X,
+                    op=ALU.add,
+                )
+
+        def value_finish(cc, d, r, c):
+            dz = dzp.tile([P, J, GT], BF16, name="dzv", tag="dz")
+            tv = cc[:].rearrange("p j (h e) -> p j h e", e=HD)
+            for q in range(2):
+                w = tmp.tile([P, 2, HH, DV], F32, name="wv", tag="t")
+                for jj in range(2):
+                    j = 2 * q + jj
+                    for h in range(HH):
+                        i = HH * j + h
+                        nc.scalar.activation(
+                            out=w[:, jj, h, :], in_=tv[:, j, h, DK:HD], func=AF.Copy, scale=c[:, 64 + i : 65 + i]
+                        )
+                        nc.vector.scalar_tensor_tensor(
+                            out=dz[:, j, DV * h : DV * (h + 1)],
+                            in0=d[:, h, j, :],
+                            scalar=r[:, 64 + i : 65 + i],
+                            in1=w[:, jj, h, :],
+                            op0=ALU.mult,
+                            op1=ALU.subtract,
+                        )
+            return dz
+
+        def qk_sums(g, hf, a, cc, qkd, ss, s_):
+            hs = slice(HH * hf, HH * (hf + 1))
+            dp = tmp.tile([P, 2, HH, J, DK], F32, name="dp", tag="t")
+            m1 = small.tile([P, 2, HH * J, 2], F32, name="m1")
+            m2 = small.tile([P, 2, HH * J, 2], F32, name="m2")
+            for s in range(2):
+                src = qkd[:, s, hs]
+                nc.gpsimd.tensor_scalar(
+                    out=dp[:, s].rearrange("p h j f -> p (h j f)"),
+                    in0=src.rearrange("p h j f -> p (h j f)"),
+                    scalar1=1.0,
+                    scalar2=0.0,
+                    op0=ALU.mult,
+                    op1=ALU.add,
+                )
+                pair = src.rearrange("p h j f -> p (h j) f")[:, :, 0:2]
+                for c, m in ((0, m1), (1, m2)):
+                    tab = cs[:, c, g, hs, :].rearrange("p h (j o) -> p (h j) o", o=1).to_broadcast([P, HH * J, 2])
+                    nc.gpsimd.tensor_tensor(out=m[:, s], in0=pair, in1=tab, op=ALU.mult)
+                dst = dp[:, s].rearrange("p h j f -> p (h j) f")
+                nc.gpsimd.tensor_tensor(out=dst[:, :, 0], in0=m1[:, s, :, 0], in1=m2[:, s, :, 1], op=ALU.add)
+                nc.gpsimd.tensor_tensor(out=dst[:, :, 1], in0=m1[:, s, :, 1], in1=m2[:, s, :, 0], op=ALU.subtract)
+            sq = tmp.tile([P, 2, J, HH, DK], F32, name="qsq", tag="t")
+            pr = tmp.tile([P, 2, J, HH, DK], F32, name="qpr", tag="t")
+            tv, dv = [], []
+            for s, t in ((0, a), (1, cc)):
+                tv.append(t[:].rearrange("p j (h e) -> p j h e", e=HD)[:, :, :, 0:DK])
+                dv.append(dp[:, s].rearrange("p h j f -> p j h f"))
+                nc.scalar.activation(out=sq[:, s], in_=tv[s], func=AF.Square)
+                nc.vector.tensor_tensor(out=pr[:, s], in0=tv[s], in1=dv[s], op=ALU.mult)
+            nc.vector.tensor_reduce(
+                out=ss[:, 0:64], in_=sq[:].rearrange("p s j h f -> p (s j h) f"), axis=AX.X, op=ALU.add
+            )
+            nc.vector.tensor_reduce(
+                out=s_[:, 0:64], in_=pr[:].rearrange("p s j h f -> p (s j h) f"), axis=AX.X, op=ALU.add
+            )
+            return tv, dv
+
+        def qk_finish(hf, tv, dv, r, c, dz0):
+            u = tmp.tile([P, 2, J, HH, DK], F32, name="qu", tag="t")
+            w = tmp.tile([P, 2, J, HH, DK], F32, name="qw", tag="t")
+            for s in range(2):
+                cols = slice(32 * s, 32 * s + 32)
+                nc.vector.tensor_tensor(out=u[:, s], in0=dv[s], in1=bcast(r[:, cols], DK), op=ALU.mult)
+                nc.vector.tensor_tensor(out=w[:, s], in0=tv[s], in1=bcast(c[:, cols], DK), op=ALU.mult)
+            nc.vector.tensor_tensor(
+                out=dz0[:].rearrange("p j (s c) -> p s j c", s=2)[:, :, :, 128 * hf : 128 * hf + 128],
+                in0=u[:].rearrange("p s j h f -> p s j (h f)"),
+                in1=w[:].rearrange("p s j h f -> p s j (h f)"),
+                op=ALU.subtract,
+            )
+
+        def token_quantise(g, which, hf, dz, dz0):
+            il = ilp.tile([P, HALF, J], BF16, name="il", tag="il", align_bytes=64)
+            rows = il[:].rearrange("p (h e) j -> p h e j", e=HD)
+            c0 = 256 * which + 128 * hf
+            nc.vector.tensor_copy(
+                out=rows[:, :, 0:DK, :], in_=dz0[:, :, c0 : c0 + 128].rearrange("p j (h f) -> p h f j", f=DK)
+            )
+            nc.vector.tensor_copy(out=rows[:, :, DK:HD, :], in_=dz[:].rearrange("p j (h f) -> p h f j", f=DV))
+            if g == 0:
+                codes = keep.tile([P, HALF], U32, name="dzc%d%d" % (which, hf), align_bytes=64)
+                scales = keep.tile([P, HALF], U8, name="dzs%d%d" % (which, hf), align_bytes=64)
+            else:
+                codes = ilp.tile([P, HALF], U32, name="dzc1", tag="dzc1", align_bytes=64)
+                scales = ilp.tile([P, HALF], U8, name="dzs1", tag="dzs1", align_bytes=64)
+            flat = il[:].rearrange("p n j -> p (n j)")
+            for lo, hi in ((0, 512), (512, 640)):
+                nc.vector.quantize_mx(
+                    out=codes[:, lo:hi].bitcast(E5M2), scales=scales[:, lo:hi], in_=flat[:, J * lo : J * hi]
+                )
+            dzc[(g, which, hf)] = (codes, scales)
+
+        turn = [0]
+
+        def evacuate(out, acc, both):
+            turn[0] += 1
+            if both and turn[0] % 2:
+                nc.vector.tensor_copy(out=out, in_=acc)
+            else:
+                nc.scalar.copy(out=out, in_=acc)
+
+        def weight_grad(which, hf, both=False):
+            dst = (out_1, out_2)[which]
+            for m in range(HALF // P):
+                res = outp.tile([P, DIM], F32, name="res", tag="res")
+                mc = slice(P * m, P * (m + 1))
+                for n in range(2):
+                    cols = slice(512 * n, 512 * (n + 1))
+                    acc = pacc.tile([P, 512], F32, name="acc", tag="acc")
+                    for g in range(2):
+                        codes, scales = dzc[(g, which, hf)]
+                        nc.tensor.matmul_mx(
+                            out=acc[:],
+                            lhsT=codes[:, mc].bitcast(E5M2),
+                            lhsT_scale=scales[:, mc],
+                            rhs=t_codes[g][:, cols].bitcast(E4M3),
+                            rhs_scale=t_scales[g][:, cols],
+                            start=(g == 0),
+                            stop=(g == 1),
+                        )
+                    evacuate(res[:, cols], acc[:], both)
+                r0 = HALF * hf + P * m
+                nc.sync.dma_start(out=dst[r0 : r0 + P, :], in_=res[:])
+
+        def token_grad_passes(g, j, n, acc, passes, first, last):
+            mc = slice(P * j, P * (j + 1))
+            cols = slice(512 * n, 512 * (n + 1))
+            for c in passes:
+                codes, scales = dzt[(g, c)]
+                nc.tensor.matmul_mx(
+                    out=acc[:],
+                    lhsT=codes[:, mc].bitcast(E5M2),
+                    lhsT_scale=scales[:, mc],
+                    rhs=w_codes[c][:, cols].bitcast(E4M3),
+                    rhs_scale=w_scales[c][:, cols],
+                    start=(c == first),
+                    stop=(c == last),
+                )
+
+        def token_grad_open(g, js, passes):
+            opened = {}
+            for j in js:
+                for n in range(2):
+                    acc = pacc.tile([P, 512], F32, name="accx", tag="acc")
+                    token_grad_passes(g, j, n, acc, passes, passes[0], None)
+                    opened[(j, n)] = acc
+            return opened
+
+        def token_grad(g, js, passes, opened, last, both=False):
+            rows = out_0[0, GT * g : GT * (g + 1), :].rearrange("(p j) w -> p j w", j=J)
+            for j in js:
+                res = outp.tile([P, DIM], F32, name="resx", tag="res")
+                for n in range(2):
+                    if (j, n) in opened:
+                        acc = opened[(j, n)]
+                        token_grad_passes(g, j, n, acc, [last], None, last)
+                    else:
+                        acc = pacc.tile([P, 512], F32, name="accx", tag="acc")
+                        token_grad_passes(g, j, n, acc, passes + [last], passes[0], last)
+                    evacuate(res[:, 512 * n : 512 * (n + 1)], acc[:], both)
+                nc.sync.dma_start(out=rows[:, j, :], in_=res[:])
+
+        qkds, dz0s = {}, {}
+
+        def load_unit(g, hf, a=None):
+            if hf == 0:
+                qkds[g] = load_qk_grads(g)
+            if a is None:
+                a = load_half(qg, g, hf)
+            d1 = load_grad(grad_1, g, hf)
+            cc = load_half(kv, g, hf)
+            d3 = load_grad(grad_3, g, hf)
+            return a, d1, cc, d3
+
+        def sums(g, hf, a, cc, d3):
+            ss = small.tile([P, 96], F32, name="ss")
+            s = small.tile([P, 96], F32, name="s")
+            tv, dv = qk_sums(g, hf, a, cc, qkds[g], ss, s)
+            value_sums(cc, d3, ss, s)
+            r, c = norm_factors(ss, s, 96)
+            return tv, dv, r, c
+
+        def unit(g, hf, a=None):
+            if hf == 0:
+                dz0s[g] = dzp.tile([P, J, GT], BF16, name="dz0", tag="dz0", bufs=1)
+            a, d1, cc, d3 = load_unit(g, hf, a)
+            if (g, hf) == (0, 0):
+                st = [gate_scalar(a, 0)]
+            tv, dv, r, c = sums(g, hf, a, cc, d3)
+            dzg = dzp.tile([P, J, GT], BF16, name="dzg", tag="dz")
+            if (g, hf) != (1, 1):
+                if (g, hf) != (0, 0):
+                    st = [gate_scalar(a, 0)]
+                st.append(gate_scalar(a, 1))
+                qk_finish(hf, tv, dv, r, c, dz0s[g])
+                dzv = value_finish(cc, d3, r, c)
+                for b in range(2):
+                    gate_vector(st[b], d1, b, dzg)
+                transpose_quantise(g, 3 + hf, dzv)
+                token_quantise(g, 1, hf, dzv, dz0s[g])
+                if g == 1:
+                    weight_grad(1, hf)
+                transpose_quantise(g, 1 + hf, dzg)
+                token_quantise(g, 0, hf, dzg, dz0s[g])
+                if g == 1:
+                    weight_grad(0, hf)
+                if hf == 1:
+                    transpose_quantise(g, 0, dz0s[g])
+            else:
+                st = [gate_scalar(a, 0)]
+                qk_finish(hf, tv, dv, r, c, dz0s[g])
+                dzv = value_finish(cc, d3, r, c)
+                transpose_quantise(g, 0, dz0s[g])
+                transpose_quantise(g, 4, dzv)
+                token_quantise(g, 1, hf, dzv, dz0s[g])
+                st.append(gate_scalar(a, 1))
+                weight_grad(1, hf)
+                gate_vector(st[0], d1, 0, dzg)
+                transpose_quantise(g, 2, dzg, (0,))
+                opened = token_grad_open(1, [0, 1], [0, 1, 3, 4])
+                gate_vector(st[1], d1, 1, dzg)
+                token_grad(1, [0, 1], None, opened, 2, True)
+                transpose_quantise(g, 2, dzg, (1,))
+                token_quantise(g, 0, hf, dzg, dz0s[g])
+                opened = token_grad_open(1, [2, 3], [0, 1, 3, 4])
+                token_grad(1, [2, 3], None, opened, 2, True)
+                weight_grad(0, hf, True)
+
+        a00 = load_half(qg, 0, 0)
+        prep_tokens(0)
+        prep_rot()
+        unit(0, 0, a00)
+        prep_weights(1)
+        prep_weights(3)
+        unit(0, 1)
+        prep_weights(0)
+        prep_weights(2)
+        prep_weights(4)
+        prep_tokens(1)
+        token_grad(0, [0, 1, 2, 3], [0, 1, 2, 3], {}, 4)
+        unit(1, 0)
+        unit(1, 1)

@@ -34,13 +34,14 @@ def tile_gatedscreeningtile_pa_v_kernel(
         const = ctx.enter_context(tc.tile_pool(name="const", bufs=1))
         ld = ctx.enter_context(tc.tile_pool(name="ld", bufs=5))
         gr = ctx.enter_context(tc.tile_pool(name="gr", bufs=5))
-        tmp = ctx.enter_context(tc.tile_pool(name="tmp", bufs=9))
+        tmp = ctx.enter_context(tc.tile_pool(name="tmp", bufs=7))
         dzp = ctx.enter_context(tc.tile_pool(name="dzp", bufs=3))
         ilp = ctx.enter_context(tc.tile_pool(name="ilp", bufs=2))
         grp = ctx.enter_context(tc.tile_pool(name="grp", bufs=3))
         keep = ctx.enter_context(tc.tile_pool(name="keep", bufs=1))
         dztp = ctx.enter_context(tc.tile_pool(name="dztp", bufs=7))
         small = ctx.enter_context(tc.tile_pool(name="small", bufs=2))
+        rotp = ctx.enter_context(tc.tile_pool(name="rotp", bufs=1))
         outp = ctx.enter_context(tc.tile_pool(name="outp", bufs=3))
         ptp = ctx.enter_context(tc.psum_pool(name="ptp", bufs=3))
         pacc = ctx.enter_context(tc.psum_pool(name="pacc", bufs=5))
@@ -52,6 +53,10 @@ def tile_gatedscreeningtile_pa_v_kernel(
         make_identity(nc, ident[:])
         ident_b = const.tile([P, P], BF16, name="ident_b")
         make_identity(nc, ident_b[:])
+        perm_b = const.tile([P, P], BF16, name="perm_b")
+        nc.vector.tensor_copy(
+            out=perm_b[:].rearrange("p (h d) -> p h d", h=HH), in_=ident_b[:].rearrange("p (d h) -> p h d", h=HH)
+        )
 
         t_codes, t_scales, w_codes, w_scales = [], [], [], []
         for g in range(2):
@@ -61,18 +66,18 @@ def tile_gatedscreeningtile_pa_v_kernel(
             w_codes.append(keep.tile([P, DIM], U32, name="w_codes%d" % c, align_bytes=64))
             w_scales.append(keep.tile([P, DIM], U8, name="w_scales%d" % c, align_bytes=64))
 
-        def interleave_quantise(raw, codes, scales, on_tensor):
+        def interleave_quantise(raw, codes, scales, mover):
             for n in range(2):
                 cols = slice(512 * n, 512 * (n + 1))
                 grouped = grp.tile([P, 512, J], BF16, name="grouped", tag="grp", align_bytes=64)
-                if on_tensor:
+                if mover is not None:
                     for k in range(2):
                         mv = ptp.tile([P, 256, J], BF16, name="mv", tag="tp")
                         for a in range(2):
                             c0 = 512 * n + 256 * k + 128 * a
                             nc.tensor.matmul(
                                 mv[:, 128 * a : 128 * (a + 1), :].rearrange("p w j -> p (w j)"),
-                                lhsT=ident_b[:],
+                                lhsT=mover[:],
                                 rhs=raw[:, :, c0 : c0 + 128].rearrange("p j w -> p w j"),
                                 start=True,
                                 stop=True,
@@ -91,7 +96,7 @@ def tile_gatedscreeningtile_pa_v_kernel(
             nc.sync.dma_start(
                 out=raw[:], in_=tokens[0, GT * g : GT * (g + 1), :].rearrange("(p j) w -> p j w", j=J)
             )
-            interleave_quantise(raw, t_codes[g], t_scales[g], g == 1)
+            interleave_quantise(raw, t_codes[g], t_scales[g], ident_b if g == 1 else None)
 
         def prep_weights(c):
             raw = ld.tile([P, J, DIM], BF16, name="raw_w", tag="ld")
@@ -99,21 +104,18 @@ def tile_gatedscreeningtile_pa_v_kernel(
             if c == 0:
                 for s, w in ((0, w_qg), (1, w_kv)):
                     heads = w.rearrange("(h e) w -> h e w", e=HD)
-                    for pp in range(4):
-                        nc.sync.dma_start(
-                            out=flat[64 * s + pp : 64 * s + 64 : 4, :],
-                            in_=heads[:, 4 * pp : 4 * pp + 4, :].rearrange("h j w -> h (j w)"),
-                        )
+                    nc.sync.dma_start(
+                        out=flat[64 * s : 64 * s + 64, :],
+                        in_=heads[:, 0:DK, :].rearrange("h (p j) w -> h p (j w)", j=J),
+                    )
             else:
                 w = w_qg if c < 3 else w_kv
                 h0 = HH * ((c - 1) % 2)
-                for hh in range(HH):
-                    r0 = HD * (h0 + hh) + DK
-                    nc.sync.dma_start(
-                        out=flat[16 * hh : 16 * hh + 16, :],
-                        in_=w[r0 : r0 + DV, :].rearrange("(p j) w -> p (j w)", j=J),
-                    )
-            interleave_quantise(raw, w_codes[c], w_scales[c], True)
+                heads = w[HD * h0 : HD * (h0 + HH), :].rearrange("(h e) w -> h e w", e=HD)
+                nc.sync.dma_start(
+                    out=flat, in_=heads[:, DK:HD, :].rearrange("h (p j) w -> p h (j w)", j=J)
+                )
+            interleave_quantise(raw, w_codes[c], w_scales[c], ident_b if c == 0 else perm_b)
 
         cs = const.tile([P, 2, 2, H, J], F32, name="cs")
 
@@ -134,10 +136,9 @@ def tile_gatedscreeningtile_pa_v_kernel(
         def load_half(src, g, hf):
             t = ld.tile([P, J, HALF], F32, name="saved", tag="ld")
             rows = src[0, GT * g : GT * (g + 1), :].rearrange("(p j) w -> p j w", j=J)
-            for lo in range(0, HALF, HALF // 2):
-                nc.sync.dma_start(
-                    out=t[:, :, lo : lo + HALF // 2], in_=rows[:, :, HALF * hf + lo : HALF * hf + lo + HALF // 2]
-                )
+            for b in range(2):
+                js = slice(2 * b, 2 * b + 2)
+                nc.sync.dma_start(out=t[:, js, :], in_=rows[:, js, HALF * hf : HALF * (hf + 1)])
             return t
 
         def load_grad(src, g, hf):
@@ -209,9 +210,9 @@ def tile_gatedscreeningtile_pa_v_kernel(
                     out=y[:], in0=z[:], scalar=1.5, in1=y[:], op0=ALU.add, op1=ALU.mult
                 )
             c = small.tile([P, n], F32, name="nc_")
-            nc.gpsimd.tensor_tensor(out=z[:], in0=y[:], in1=y[:], op=ALU.mult)
-            nc.gpsimd.tensor_tensor(out=c[:], in0=y[:], in1=s[:], op=ALU.mult)
-            nc.gpsimd.tensor_tensor(out=c[:], in0=c[:], in1=z[:], op=ALU.mult)
+            nc.vector.tensor_tensor(out=z[:], in0=y[:], in1=y[:], op=ALU.mult)
+            nc.vector.tensor_tensor(out=c[:], in0=y[:], in1=s[:], op=ALU.mult)
+            nc.vector.tensor_tensor(out=c[:], in0=c[:], in1=z[:], op=ALU.mult)
             return y, c
 
         def gate_scalar(a, b):
@@ -288,34 +289,39 @@ def tile_gatedscreeningtile_pa_v_kernel(
                         )
             return dz
 
-        def qk_sums(g, hf, a, cc, qkd, ss, s_):
-            hs = slice(HH * hf, HH * (hf + 1))
-            dp = tmp.tile([P, 2, HH, J, DK], F32, name="dp", tag="t")
-            m1 = small.tile([P, 2, HH * J, 2], F32, name="m1")
-            m2 = small.tile([P, 2, HH * J, 2], F32, name="m2")
-            for s in range(2):
-                src = qkd[:, s, hs]
-                nc.gpsimd.tensor_scalar(
-                    out=dp[:, s].rearrange("p h j f -> p (h j f)"),
-                    in0=src.rearrange("p h j f -> p (h j f)"),
-                    scalar1=1.0,
-                    scalar2=0.0,
-                    op0=ALU.mult,
-                    op1=ALU.add,
+        def rotate_back(g, d):
+            dp = rotp.tile([P, 2, H, J, DK], F32, name="dp")
+            nc.scalar.activation(
+                out=dp[:].rearrange("p s h j f -> p (s h j f)"),
+                in_=d[:].rearrange("p s h j f -> p (s h j f)"),
+                func=AF.Copy,
+            )
+            pair = d[:].rearrange("p s h j f -> p s (h j) f")[:, :, :, 0:2]
+            m = []
+            for c in range(2):
+                mc = rotp.tile([P, 2, H * J, 2], F32, name="m%d" % c)
+                tab = cs[:, c, g].rearrange("p (o h) (j t) -> p o (h j) t", o=1, t=1)
+                nc.vector.tensor_tensor(
+                    out=mc[:], in0=pair, in1=tab.to_broadcast([P, 2, H * J, 2]), op=ALU.mult
                 )
-                pair = src.rearrange("p h j f -> p (h j) f")[:, :, 0:2]
-                for c, m in ((0, m1), (1, m2)):
-                    tab = cs[:, c, g, hs, :].rearrange("p h (j o) -> p (h j) o", o=1).to_broadcast([P, HH * J, 2])
-                    nc.gpsimd.tensor_tensor(out=m[:, s], in0=pair, in1=tab, op=ALU.mult)
-                dst = dp[:, s].rearrange("p h j f -> p (h j) f")
-                nc.gpsimd.tensor_tensor(out=dst[:, :, 0], in0=m1[:, s, :, 0], in1=m2[:, s, :, 1], op=ALU.add)
-                nc.gpsimd.tensor_tensor(out=dst[:, :, 1], in0=m1[:, s, :, 1], in1=m2[:, s, :, 0], op=ALU.subtract)
+                m.append(mc)
+            dst = dp[:].rearrange("p s h j f -> p s (h j) f")
+            nc.vector.tensor_tensor(
+                out=dst[:, :, :, 0], in0=m[0][:, :, :, 0], in1=m[1][:, :, :, 1], op=ALU.add
+            )
+            nc.vector.tensor_tensor(
+                out=dst[:, :, :, 1], in0=m[0][:, :, :, 1], in1=m[1][:, :, :, 0], op=ALU.subtract
+            )
+            return dp
+
+        def qk_sums(g, hf, a, cc, dp, ss, s_):
+            hs = slice(HH * hf, HH * (hf + 1))
             sq = tmp.tile([P, 2, J, HH, DK], F32, name="qsq", tag="t")
             pr = tmp.tile([P, 2, J, HH, DK], F32, name="qpr", tag="t")
             tv, dv = [], []
             for s, t in ((0, a), (1, cc)):
                 tv.append(t[:].rearrange("p j (h e) -> p j h e", e=HD)[:, :, :, 0:DK])
-                dv.append(dp[:, s].rearrange("p h j f -> p j h f"))
+                dv.append(dp[:, s, hs].rearrange("p h j f -> p j h f"))
                 nc.scalar.activation(out=sq[:, s], in_=tv[s], func=AF.Square)
                 nc.vector.tensor_tensor(out=pr[:, s], in0=tv[s], in1=dv[s], op=ALU.mult)
             nc.vector.tensor_reduce(
@@ -431,22 +437,22 @@ def tile_gatedscreeningtile_pa_v_kernel(
                     evacuate(res[:, 512 * n : 512 * (n + 1)], acc[:], both)
                 nc.sync.dma_start(out=rows[:, j, :], in_=res[:])
 
-        qkds, dz0s = {}, {}
+        qkds, dz0s, dps = {}, {}, {}
 
         def load_unit(g, hf, a=None):
-            if hf == 0:
-                qkds[g] = load_qk_grads(g)
             if a is None:
                 a = load_half(qg, g, hf)
-            d1 = load_grad(grad_1, g, hf)
             cc = load_half(kv, g, hf)
             d3 = load_grad(grad_3, g, hf)
+            if hf == 0:
+                qkds[g] = load_qk_grads(g)
+            d1 = load_grad(grad_1, g, hf)
             return a, d1, cc, d3
 
         def sums(g, hf, a, cc, d3):
             ss = small.tile([P, 96], F32, name="ss")
             s = small.tile([P, 96], F32, name="s")
-            tv, dv = qk_sums(g, hf, a, cc, qkds[g], ss, s)
+            tv, dv = qk_sums(g, hf, a, cc, dps[g], ss, s)
             value_sums(cc, d3, ss, s)
             r, c = norm_factors(ss, s, 96)
             return tv, dv, r, c
@@ -457,6 +463,9 @@ def tile_gatedscreeningtile_pa_v_kernel(
             a, d1, cc, d3 = load_unit(g, hf, a)
             if (g, hf) == (0, 0):
                 st = [gate_scalar(a, 0)]
+                prep_rot()
+            if hf == 0:
+                dps[g] = rotate_back(g, qkds[g])
             tv, dv, r, c = sums(g, hf, a, cc, d3)
             dzg = dzp.tile([P, J, GT], BF16, name="dzg", tag="dz")
             if (g, hf) != (1, 1):
@@ -499,7 +508,6 @@ def tile_gatedscreeningtile_pa_v_kernel(
 
         a00 = load_half(qg, 0, 0)
         prep_tokens(0)
-        prep_rot()
         unit(0, 0, a00)
         prep_weights(1)
         prep_weights(3)

@@ -1,4 +1,5 @@
 from contextlib import ExitStack
+from functools import partial
 
 import concourse.mybir as mybir
 from concourse.masks import make_identity
@@ -10,20 +11,22 @@ FLOPS = 2 * 2 * N * (2 * DI) * DIM
 
 F32 = mybir.dt.float32
 BF16 = mybir.dt.bfloat16
+I32 = mybir.dt.int32
 U32 = mybir.dt.uint32
 U8 = mybir.dt.uint8
-I32 = mybir.dt.int32
 E4M3 = mybir.dt.float8_e4m3fn_x4
 E5M2 = mybir.dt.float8_e5m2_x4
 AF = mybir.ActivationFunctionType
 ALU = mybir.AluOpType
 AX = mybir.AxisListType
+ENGINES = mybir.EngineType
 
 P = 128
 J = 4
 GT = 512
 HH = 8
 HALF = HH * HD
+UNITS = ((0, 0), (0, 1), (1, 0), (1, 1))
 
 
 def tile_gatedscreeningtile_pa_v_kernel(
@@ -32,23 +35,26 @@ def tile_gatedscreeningtile_pa_v_kernel(
     nc = tc.nc
     with ExitStack() as ctx:
         const = ctx.enter_context(tc.tile_pool(name="const", bufs=1))
-        ld = ctx.enter_context(tc.tile_pool(name="ld", bufs=5))
+        ld = ctx.enter_context(tc.tile_pool(name="ld", bufs=4))
+        io = ctx.enter_context(tc.tile_pool(name="io", bufs=4))
         gr = ctx.enter_context(tc.tile_pool(name="gr", bufs=5))
-        tmp = ctx.enter_context(tc.tile_pool(name="tmp", bufs=7))
+        tmp = ctx.enter_context(tc.tile_pool(name="tmp", bufs=10))
         dzp = ctx.enter_context(tc.tile_pool(name="dzp", bufs=3))
-        ilp = ctx.enter_context(tc.tile_pool(name="ilp", bufs=2))
-        grp = ctx.enter_context(tc.tile_pool(name="grp", bufs=3))
+        ilp = ctx.enter_context(tc.tile_pool(name="ilp", bufs=3))
+        grp = ctx.enter_context(tc.tile_pool(name="grp", bufs=2))
+        dzcp = ctx.enter_context(tc.tile_pool(name="dzcp", bufs=2))
         keep = ctx.enter_context(tc.tile_pool(name="keep", bufs=1))
-        dztp = ctx.enter_context(tc.tile_pool(name="dztp", bufs=7))
+        dztp = ctx.enter_context(tc.tile_pool(name="dztp", bufs=6))
         small = ctx.enter_context(tc.tile_pool(name="small", bufs=2))
         rotp = ctx.enter_context(tc.tile_pool(name="rotp", bufs=1))
-        outp = ctx.enter_context(tc.tile_pool(name="outp", bufs=3))
-        ptp = ctx.enter_context(tc.psum_pool(name="ptp", bufs=3))
-        pacc = ctx.enter_context(tc.psum_pool(name="pacc", bufs=5))
+        ptp = ctx.enter_context(tc.psum_pool(name="ptp", bufs=2))
+        pacc = ctx.enter_context(tc.psum_pool(name="pacc", bufs=6))
+        ctx.enter_context(tc.manual_schedule(engines={ENGINES.DVE, ENGINES.Activation, ENGINES.PE}))
 
         warm = const.tile([P, 1], F32, name="warm")
         nc.vector.memset(warm[:], 0.0)
         nc.scalar.activation(out=warm[:], in_=warm[:], func=AF.Silu)
+        junk = const.tile([P, HH, DV], BF16, name="junk")
         ident = const.tile([P, P], F32, name="ident")
         make_identity(nc, ident[:])
         ident_b = const.tile([P, P], BF16, name="ident_b")
@@ -57,6 +63,7 @@ def tile_gatedscreeningtile_pa_v_kernel(
         nc.vector.tensor_copy(
             out=perm_b[:].rearrange("p (h d) -> p h d", h=HH), in_=ident_b[:].rearrange("p (d h) -> p h d", h=HH)
         )
+        cs = const.tile([P, 2, 2, H, J], F32, name="cs")
 
         t_codes, t_scales, w_codes, w_scales = [], [], [], []
         for g in range(2):
@@ -66,74 +73,108 @@ def tile_gatedscreeningtile_pa_v_kernel(
             w_codes.append(keep.tile([P, DIM], U32, name="w_codes%d" % c, align_bytes=64))
             w_scales.append(keep.tile([P, DIM], U8, name="w_scales%d" % c, align_bytes=64))
 
-        def interleave_quantise(raw, codes, scales, mover):
-            for n in range(2):
-                cols = slice(512 * n, 512 * (n + 1))
-                grouped = grp.tile([P, 512, J], BF16, name="grouped", tag="grp", align_bytes=64)
-                if mover is not None:
-                    for k in range(2):
-                        mv = ptp.tile([P, 256, J], BF16, name="mv", tag="tp")
-                        for a in range(2):
-                            c0 = 512 * n + 256 * k + 128 * a
-                            nc.tensor.matmul(
-                                mv[:, 128 * a : 128 * (a + 1), :].rearrange("p w j -> p (w j)"),
-                                lhsT=mover[:],
-                                rhs=raw[:, :, c0 : c0 + 128].rearrange("p j w -> p w j"),
-                                start=True,
-                                stop=True,
-                            )
-                        nc.scalar.copy(out=grouped[:, 256 * k : 256 * (k + 1), :], in_=mv[:])
+        def drain(steps):
+            while steps:
+                steps.pop(0)()
+
+        def weave(main, filler):
+            for step in main:
+                step()
+                if filler:
+                    filler.pop(0)()
+
+        def load_tokens(g, whole=False):
+            rows = tokens[0, GT * g : GT * (g + 1), :].rearrange("(p j) w -> p j w", j=J)
+            if whole:
+                raw = ld.tile([P, J, DIM], BF16, name="raw_t0", tag="ld")
+                for n in range(2):
+                    cols = slice(512 * n, 512 * (n + 1))
+                    nc.sync.dma_start(out=raw[:, :, cols], in_=rows[:, :, cols])
+                return raw
+            raw = []
+            for b in range(2):
+                raw.append(io.tile([P, 2, DIM], BF16, name="raw_t", tag="io"))
+                nc.sync.dma_start(out=raw[b][:], in_=rows[:, 2 * b : 2 * b + 2, :])
+            return raw
+
+        def load_weights(c):
+            raw = []
+            for b in range(2):
+                raw.append(io.tile([P, 2, DIM], BF16, name="raw_w", tag="io"))
+                flat = raw[b][:].rearrange("p j w -> p (j w)")
+                js = slice(2 * b, 2 * b + 2)
+                if c == 0:
+                    for s, w in ((0, w_qg), (1, w_kv)):
+                        heads = w.rearrange("(h e) w -> h e w", e=HD)[:, 0:DK, :]
+                        nc.sync.dma_start(
+                            out=flat[64 * s : 64 * s + 64, :],
+                            in_=heads.rearrange("h (p j) w -> h p j w", j=J)[:, :, js, :].rearrange("h p j w -> h p (j w)"),
+                        )
                 else:
-                    nc.vector.tensor_copy(out=grouped[:], in_=raw[:, :, cols].rearrange("p j w -> p w j"))
-                nc.vector.quantize_mx(
-                    out=codes[:, cols].bitcast(E4M3),
-                    scales=scales[:, cols],
-                    in_=grouped[:].rearrange("p w j -> p (w j)"),
-                )
-
-        def prep_tokens(g):
-            raw = ld.tile([P, J, DIM], BF16, name="raw_t", tag="ld")
-            nc.sync.dma_start(
-                out=raw[:], in_=tokens[0, GT * g : GT * (g + 1), :].rearrange("(p j) w -> p j w", j=J)
-            )
-            interleave_quantise(raw, t_codes[g], t_scales[g], ident_b if g == 1 else None)
-
-        def prep_weights(c):
-            raw = ld.tile([P, J, DIM], BF16, name="raw_w", tag="ld")
-            flat = raw[:].rearrange("p j w -> p (j w)")
-            if c == 0:
-                for s, w in ((0, w_qg), (1, w_kv)):
-                    heads = w.rearrange("(h e) w -> h e w", e=HD)
+                    w = w_qg if c < 3 else w_kv
+                    h0 = HH * ((c - 1) % 2)
+                    heads = w[HD * h0 : HD * (h0 + HH), :].rearrange("(h e) w -> h e w", e=HD)[:, DK:HD, :]
                     nc.sync.dma_start(
-                        out=flat[64 * s : 64 * s + 64, :],
-                        in_=heads[:, 0:DK, :].rearrange("h (p j) w -> h p (j w)", j=J),
+                        out=flat,
+                        in_=heads.rearrange("h (p j) w -> p h j w", j=J)[:, :, js, :].rearrange("p h j w -> p h (j w)"),
                     )
-            else:
-                w = w_qg if c < 3 else w_kv
-                h0 = HH * ((c - 1) % 2)
-                heads = w[HD * h0 : HD * (h0 + HH), :].rearrange("(h e) w -> h e w", e=HD)
-                nc.sync.dma_start(
-                    out=flat, in_=heads[:, DK:HD, :].rearrange("h (p j) w -> p h (j w)", j=J)
-                )
-            interleave_quantise(raw, w_codes[c], w_scales[c], ident_b if c == 0 else perm_b)
+            return raw
 
-        cs = const.tile([P, 2, 2, H, J], F32, name="cs")
+        def quantise_piece(grouped, codes, scales, n):
+            cols = slice(512 * n, 512 * (n + 1))
+            nc.vector.quantize_mx(
+                out=codes[:, cols].bitcast(E4M3),
+                scales=scales[:, cols],
+                in_=grouped[:, 0:512, :].rearrange("p w j -> p (w j)"),
+            )
 
-        def prep_rot():
-            rt = const.tile([P, GT], F32, name="rt")
-            nc.vector.memset(rt[64:128, :], 0.0)
-            nc.sync.dma_start(out=rt[0:64, :], in_=rot.rearrange("c h (g n) -> (c h g) n", g=2))
-            rp = ptp.tile([P, J, P], F32, name="rp", tag="tp")
-            for j in range(J):
-                nc.tensor.transpose(rp[:, j, :], rt[:, j::J], ident[:])
-            for c in range(2):
-                for g in range(2):
-                    nc.scalar.copy(
-                        out=cs[:, c, g, :, :],
-                        in_=rp[:, :, 32 * c : 32 * c + 32].rearrange("p j (h g) -> p g h j", g=2)[:, g, :, :],
+        def group_on_vector(raw, n):
+            grouped = ilp.tile([P, HALF, J], BF16, name="grouped_v", tag="il", align_bytes=64)
+            nc.vector.tensor_copy(
+                out=grouped[:, 0:512, :], in_=raw[:, :, 512 * n : 512 * (n + 1)].rearrange("p j w -> p w j")
+            )
+            return grouped
+
+        def group_on_tensor(raw, n, mover):
+            grouped = grp.tile([P, 512, J], BF16, name="grouped_t", tag="grp", align_bytes=64)
+            for k in range(2):
+                mv = pacc.tile([P, 256, J], BF16, name="mv", tag="acc")
+                c0 = 512 * n + 256 * k
+                for b in range(2):
+                    nc.tensor.matmul(
+                        mv[:, :, 2 * b : 2 * b + 2],
+                        lhsT=mover[:],
+                        rhs=raw[b][:, :, c0 : c0 + 256].rearrange("p j w -> p w j"),
+                        start=True,
+                        stop=True,
                     )
+                nc.scalar.copy(out=grouped[:, 256 * k : 256 * (k + 1), :], in_=mv[:])
+            return grouped
 
-        def load_half(src, g, hf):
+        order = [("w", 1), ("w", 2), ("w", 3), ("w", 4), ("w", 0), ("t", 1)]
+        raws = {}
+        pending = []
+
+        def load_raw(kind, c):
+            raws[(kind, c)] = load_weights(c) if kind == "w" else load_tokens(c)
+
+        def prepare(i, n):
+            kind, c = order[i]
+            if n == 0 and i + 1 < len(order):
+                load_raw(*order[i + 1])
+            codes, scales = (w_codes[c], w_scales[c]) if kind == "w" else (t_codes[c], t_scales[c])
+            mover = perm_b if kind == "w" and c > 0 else ident_b
+            pending.append((group_on_tensor(raws[(kind, c)], n, mover), codes, scales, n))
+
+        def settle():
+            if pending:
+                quantise_piece(*pending.pop(0))
+
+        ua, uc, ud1, ud3, uqk, urot, udz0 = {}, {}, {}, {}, {}, {}, {}
+        usum, ufac, ugate, udzg, udzv, uw = {}, {}, {}, {}, {}, {}
+        dzt, dzc = {}, {}
+
+        def load_saved(src, g, hf):
             t = ld.tile([P, J, HALF], F32, name="saved", tag="ld")
             rows = src[0, GT * g : GT * (g + 1), :].rearrange("(p j) w -> p j w", j=J)
             for b in range(2):
@@ -149,25 +190,258 @@ def tile_gatedscreeningtile_pa_v_kernel(
             )
             return t
 
-        def load_qk_grads(g):
+        def load_qk(g):
             t = gr.tile([P, 2, H, J, DK], BF16, name="qkgrad", tag="gr")
             for s, src in ((0, grad_0), (1, grad_2)):
                 nc.sync.dma_start(
                     out=t[:, s].rearrange("p h j f -> p h (j f)"),
                     in_=src[0, :, GT * g : GT * (g + 1), :].rearrange("h (p j) f -> p h (j f)", j=J),
                 )
-            return t
+            uqk[g] = t
 
-        dzt = {}
-        dzc = {}
+        def load_unit(k):
+            g, hf = UNITS[k]
+            ua[k] = load_saved(qg, g, hf)
+            uc[k] = load_saved(kv, g, hf)
+            ud3[k] = load_grad(grad_3, g, hf)
+            if hf == 0:
+                load_qk(g)
+            ud1[k] = load_grad(grad_1, g, hf)
 
-        def transpose_quantise(g, c, dz, bs=(0, 1)):
+        def heads_of(t):
+            return t[:].rearrange("p j (h e) -> p j h e", e=HD)
+
+        def prep_rot():
+            rt = tmp.tile([P, 2, GT], F32, name="rt", tag="t")
+            nc.vector.memset(rt[64:128, 0, :], 0.0)
+            nc.sync.dma_start(out=rt[0:64, 0, :], in_=rot.rearrange("c h (g n) -> (c h g) n", g=2))
+            rp = ptp.tile([P, J, P], F32, name="rp", tag="tp")
+            for j in range(J):
+                nc.tensor.transpose(rp[:, j, :], rt[:, 0, j::J], ident[:])
+            for c in range(2):
+                for g in range(2):
+                    nc.scalar.copy(
+                        out=cs[:, c, g, :, :],
+                        in_=rp[:, :, 32 * c : 32 * c + 32].rearrange("p j (h g) -> p g h j", g=2)[:, g, :, :],
+                    )
+
+        def cast_back(k):
+            g, hf = UNITS[k]
+            dp = rotp.tile([P, 2, HH, J, DK], F32, name="dp")
+            nc.scalar.activation(
+                out=dp[:].rearrange("p s h j f -> p s (h j f)"),
+                in_=uqk[g][:, :, HH * hf : HH * (hf + 1)].rearrange("p s h j f -> p s (h j f)"),
+                func=AF.Copy,
+            )
+            urot[k] = dp
+
+        def rotate_back(k):
+            g, hf = UNITS[k]
+            hs = slice(HH * hf, HH * (hf + 1))
+            pair = uqk[g][:, :, hs].rearrange("p s h j f -> p s (h j) f")[:, :, :, 0:2]
+            steps, m = [], []
+            for c in range(2):
+                mc = small.tile([P, 2, HH * J, 2], F32, name="m%d" % c)
+                tab = cs[:, c, g, hs].rearrange("p (o h) (j t) -> p o (h j) t", o=1, t=1)
+                tab = tab.to_broadcast([P, 2, HH * J, 2])
+                steps.append(partial(nc.vector.tensor_tensor, out=mc[:], in0=pair, in1=tab, op=ALU.mult))
+                m.append(mc)
+            dst = urot[k][:].rearrange("p s h j f -> p s (h j) f")
+            for i, op in ((0, ALU.add), (1, ALU.subtract)):
+                steps.append(
+                    partial(
+                        nc.vector.tensor_tensor,
+                        out=dst[:, :, :, i],
+                        in0=m[0][:, :, :, i],
+                        in1=m[1][:, :, :, 1 - i],
+                        op=op,
+                    )
+                )
+            return steps
+
+        def squares(k):
+            ss = small.tile([P, 96], F32, name="ss")
+            s = small.tile([P, 96], F32, name="s")
+            sq = tmp.tile([P, 2, J, HH, DK], F32, name="qsq", tag="t")
+            for i, t in enumerate((ua[k], uc[k])):
+                nc.scalar.activation(out=sq[:, i], in_=heads_of(t)[:, :, :, 0:DK], func=AF.Square)
+            for j in range(J):
+                for h in range(HH):
+                    i = 64 + HH * j + h
+                    nc.scalar.activation(
+                        out=junk[:, h, :], in_=heads_of(uc[k])[:, j, h, DK:HD], func=AF.Square, accum_out=ss[:, i : i + 1]
+                    )
+            usum[k] = (ss, s, sq)
+
+        def rotated(k, s):
+            return urot[k][:, s].rearrange("p h j f -> p j h f")
+
+        def products(k):
+            ss, s, sq = usum[k]
+            dv = ud3[k][:].rearrange("p h j f -> p j h f")
+            tv = heads_of(uc[k])
+            pr = tmp.tile([P, 2, J, HH, DK], F32, name="qpr", tag="t")
+            steps, sums = [], []
+            for i in range(2):
+                js = slice(2 * i, 2 * i + 2)
+                pv = tmp.tile([P, 2, HH, DV], F32, name="pv", tag="t")
+                steps.append(
+                    partial(nc.vector.tensor_tensor, out=pv[:], in0=tv[:, js, :, DK:HD], in1=dv[:, js], op=ALU.mult)
+                )
+                sums.append((pv[:].rearrange("p j h f -> p (j h) f"), s[:, 64 + 16 * i : 80 + 16 * i]))
+            for i, t in enumerate((ua[k], uc[k])):
+                steps.append(
+                    partial(
+                        nc.vector.tensor_tensor,
+                        out=pr[:, i],
+                        in0=heads_of(t)[:, :, :, 0:DK],
+                        in1=rotated(k, i),
+                        op=ALU.mult,
+                    )
+                )
+            sums.append((pr[:].rearrange("p s j h f -> p (s j h) f"), s[:, 0:64]))
+            sums.append((sq[:].rearrange("p s j h f -> p (s j h) f"), ss[:, 0:64]))
+            for src, dst in sums:
+                steps.append(partial(nc.vector.tensor_reduce, out=dst, in_=src, axis=AX.X, op=ALU.add))
+            return steps
+
+        def factors(k):
+            ss, s, _ = usum[k]
+            x = small.tile([P, 96], F32, name="nx")
+            y = small.tile([P, 96], F32, name="ny")
+            z = small.tile([P, 96], F32, name="nz")
+            c = small.tile([P, 96], F32, name="nc_")
+            ufac[k] = (y, c)
+            yi = y[:].bitcast(I32)
+            ts, tt, stt = nc.vector.tensor_scalar, nc.vector.tensor_tensor, nc.vector.scalar_tensor_tensor
+            steps = [
+                partial(ts, out=x[:], in0=ss[:], scalar1=1e-24, scalar2=None, op0=ALU.max),
+                partial(ts, out=yi, in0=x[:].bitcast(I32), scalar1=1, scalar2=None, op0=ALU.arith_shift_right),
+                partial(ts, out=yi, in0=yi, scalar1=-1.0, scalar2=1597463007.0, op0=ALU.mult, op1=ALU.add),
+            ]
+            for it in range(3):
+                steps += [
+                    partial(tt, out=z[:], in0=y[:], in1=y[:], op=ALU.mult),
+                    partial(stt, out=z[:], in0=z[:], scalar=-0.5, in1=x[:], op0=ALU.mult, op1=ALU.mult),
+                    partial(stt, out=y[:], in0=z[:], scalar=1.5, in1=y[:], op0=ALU.add, op1=ALU.mult),
+                ]
+            steps += [
+                partial(tt, out=z[:], in0=y[:], in1=y[:], op=ALU.mult),
+                partial(tt, out=c[:], in0=y[:], in1=s[:], op=ALU.mult),
+                partial(tt, out=c[:], in0=c[:], in1=z[:], op=ALU.mult),
+            ]
+            return steps
+
+        def corrections(k):
+            _, c = ufac[k]
+            uw[k] = []
+            for q in range(2):
+                w = tmp.tile([P, 2, HH, DV], F32, name="wv", tag="t")
+                uw[k].append(w)
+                for jj in range(2):
+                    for h in range(HH):
+                        i = 64 + HH * (2 * q + jj) + h
+                        nc.scalar.activation(
+                            out=w[:, jj, h, :],
+                            in_=heads_of(uc[k])[:, 2 * q + jj, h, DK:HD],
+                            func=AF.Copy,
+                            scale=c[:, i : i + 1],
+                        )
+
+        def bcast(ap):
+            return ap.rearrange("p (j h o) -> p j h o", h=HH, o=1).to_broadcast([P, J, HH, DK])
+
+        def finish_qk(k):
+            y, c = ufac[k]
+            qu = tmp.tile([P, 2, J, HH, DK], F32, name="qu", tag="t")
+            qw = tmp.tile([P, 2, J, HH, DK], F32, name="qw", tag="t")
+            for s, t in enumerate((ua[k], uc[k])):
+                cols = slice(32 * s, 32 * s + 32)
+                nc.vector.tensor_tensor(out=qu[:, s], in0=rotated(k, s), in1=bcast(y[:, cols]), op=ALU.mult)
+                nc.vector.tensor_tensor(
+                    out=qw[:, s], in0=heads_of(t)[:, :, :, 0:DK], in1=bcast(c[:, cols]), op=ALU.mult
+                )
+            return qu, qw
+
+        def finish_v(k, q):
+            y, _ = ufac[k]
+            for jj in range(2):
+                j = 2 * q + jj
+                for h in range(HH):
+                    i = 64 + HH * j + h
+                    nc.vector.scalar_tensor_tensor(
+                        out=udzv[k][:, j, DV * h : DV * (h + 1)],
+                        in0=ud3[k][:, h, j, :],
+                        scalar=y[:, i : i + 1],
+                        in1=uw[k][q][:, jj, h, :],
+                        op0=ALU.mult,
+                        op1=ALU.subtract,
+                    )
+
+        def finish(k):
+            g, hf = UNITS[k]
+            if hf == 0:
+                udz0[g] = dzp.tile([P, J, GT], BF16, name="dz0", tag="dz0", bufs=1)
+            qu, qw = finish_qk(k)
+            udzv[k] = dzp.tile([P, J, GT], BF16, name="dzv", tag="dz")
+            finish_v(k, 0)
+            nc.vector.tensor_tensor(
+                out=udz0[g][:].rearrange("p j (s c) -> p s j c", s=2)[:, :, :, 128 * hf : 128 * hf + 128],
+                in0=qu[:].rearrange("p s j h f -> p s j (h f)"),
+                in1=qw[:].rearrange("p s j h f -> p s j (h f)"),
+                op=ALU.subtract,
+            )
+            finish_v(k, 1)
+
+        def gate_scalar(k, b):
+            gv = ua[k][:].rearrange("p j (h e) -> p h j e", e=HD)[:, :, 2 * b : 2 * b + 2, DK:HD]
+            u = tmp.tile([P, HH, 2, DV], F32, name="gu", tag="t")
+            nc.scalar.activation(out=u[:], in_=gv, func=AF.Silu)
+            hh = tmp.tile([P, HH, 2, DV], F32, name="gh", tag="t")
+            nc.scalar.activation(out=hh[:], in_=gv, func=AF.Tanh, scale=0.5)
+            th = tmp.tile([P, HH, 2, DV], F32, name="gth", tag="t")
+            nc.scalar.activation(out=th[:], in_=u[:], func=AF.Tanh)
+            nc.scalar.activation(out=u[:], in_=u[:], func=AF.Copy, scale=0.5, bias=-0.5)
+            nc.scalar.activation(out=th[:], in_=th[:], func=AF.Square)
+            ugate[(k, b)] = (hh, u, th)
+
+        def gate_m(k, b):
+            hh, u, _ = ugate[(k, b)]
+            nc.vector.scalar_tensor_tensor(out=u[:], in0=hh[:], scalar=1.0, in1=u[:], op0=ALU.subtract, op1=ALU.mult)
+
+        def gate_k(k, b):
+            _, u, _ = ugate[(k, b)]
+            d = ud1[k][:, :, 2 * b : 2 * b + 2, :]
+            nc.vector.scalar_tensor_tensor(out=u[:], in0=u[:], scalar=1.0, in1=d, op0=ALU.subtract, op1=ALU.mult)
+
+        def gate_dz(k, b, jj):
+            if k not in udzg:
+                udzg[k] = dzp.tile([P, J, GT], BF16, name="dzg", tag="dz")
+            _, u, th = ugate[(k, b)]
+            nc.vector.scalar_tensor_tensor(
+                out=udzg[k][:, 2 * b + jj, :].rearrange("p (h f) -> p h f", f=DV),
+                in0=th[:, :, jj, :],
+                scalar=1.0,
+                in1=u[:, :, jj, :],
+                op0=ALU.subtract,
+                op1=ALU.mult,
+            )
+
+        def gate_head(k, bs):
+            return [partial(gate_m, k, b) for b in bs] + [partial(gate_k, k, b) for b in bs]
+
+        def gate_tail(k, bs):
+            return [partial(gate_dz, k, b, jj) for b in bs for jj in range(2)]
+
+        groupt = {}
+
+        def transpose_features(g, c, dz, bs=(0, 1)):
             if (g, c) not in dzt:
                 codes = dztp.tile([P, GT], U32, name="dzt_codes", tag="dztc", align_bytes=64)
                 scales = dztp.tile([P, GT], U8, name="dzt_scales", tag="dzts", align_bytes=64)
                 dzt[(g, c)] = (codes, scales)
-            codes, scales = dzt[(g, c)]
-            grouped = grp.tile([P, GT, J], BF16, name="groupedt", tag="grp", align_bytes=64)
+            grouped = ilp.tile([P, HALF, J], BF16, name="groupedt", tag="il", align_bytes=64)
+            groupt[(g, c)] = grouped
             gw = grouped[:].rearrange("p n t -> p (n t)").bitcast(F32)
             for b in bs:
                 tp = ptp.tile([P, 2, 2, P], F32, name="tp", tag="tp")
@@ -179,195 +453,62 @@ def tile_gatedscreeningtile_pa_v_kernel(
                     out=gw[:, 512 * b : 512 * (b + 1)].rearrange("p (j r u) -> p j r u", j=2, u=2),
                     in_=tp[:].rearrange("p j u r -> p j r u"),
                 )
+
+        def quantise_columns(g, c, bs):
+            codes, scales = dzt[(g, c)]
             cols = slice(256 * bs[0], 256 * (bs[-1] + 1))
             nc.vector.quantize_mx(
                 out=codes[:, cols].bitcast(E5M2),
                 scales=scales[:, cols],
-                in_=grouped[:, cols, :].rearrange("p n t -> p (n t)"),
+                in_=groupt[(g, c)][:, cols, :].rearrange("p n t -> p (n t)"),
             )
 
-        def bcast(ap, n):
-            return ap.rearrange("p (j h o) -> p j h o", h=HH, o=1).to_broadcast([P, J, HH, n])
+        def quantise_features(g, c, bs=(0, 1)):
+            return [partial(quantise_columns, g, c, bs)]
 
-        def norm_factors(ss, s, n):
-            x = small.tile([P, n], F32, name="nx")
-            nc.vector.tensor_scalar(out=x[:], in0=ss[:], scalar1=1e-24, scalar2=None, op0=ALU.max)
-            y = small.tile([P, n], F32, name="ny")
-            yi = y[:].bitcast(I32)
-            nc.vector.tensor_scalar(
-                out=yi, in0=x[:].bitcast(I32), scalar1=1, scalar2=None, op0=ALU.arith_shift_right
-            )
-            nc.vector.tensor_scalar(
-                out=yi, in0=yi, scalar1=-1.0, scalar2=1597463007.0, op0=ALU.mult, op1=ALU.add
-            )
-            z = small.tile([P, n], F32, name="nz")
-            for it in range(3):
-                nc.vector.tensor_tensor(out=z[:], in0=y[:], in1=y[:], op=ALU.mult)
-                nc.vector.scalar_tensor_tensor(
-                    out=z[:], in0=z[:], scalar=-0.5, in1=x[:], op0=ALU.mult, op1=ALU.mult
-                )
-                nc.vector.scalar_tensor_tensor(
-                    out=y[:], in0=z[:], scalar=1.5, in1=y[:], op0=ALU.add, op1=ALU.mult
-                )
-            c = small.tile([P, n], F32, name="nc_")
-            nc.vector.tensor_tensor(out=z[:], in0=y[:], in1=y[:], op=ALU.mult)
-            nc.vector.tensor_tensor(out=c[:], in0=y[:], in1=s[:], op=ALU.mult)
-            nc.vector.tensor_tensor(out=c[:], in0=c[:], in1=z[:], op=ALU.mult)
-            return y, c
+        uil = {}
 
-        def gate_scalar(a, b):
-            js = slice(2 * b, 2 * b + 2)
-            gv = a[:].rearrange("p j (h e) -> p h j e", e=HD)[:, :, js, DK:HD]
-            hh = tmp.tile([P, HH, 2, DV], F32, name="gh", tag="t")
-            nc.scalar.activation(out=hh[:], in_=gv, func=AF.Tanh, scale=0.5)
-            u = tmp.tile([P, HH, 2, DV], F32, name="gu", tag="t")
-            nc.scalar.activation(out=u[:], in_=gv, func=AF.Silu)
-            th = tmp.tile([P, HH, 2, DV], F32, name="gth", tag="t")
-            nc.scalar.activation(out=th[:], in_=u[:], func=AF.Tanh)
-            nc.scalar.activation(out=u[:], in_=u[:], func=AF.Copy, scale=0.5, bias=-0.5)
-            nc.scalar.activation(out=th[:], in_=th[:], func=AF.Square)
-            return hh, u, th
-
-        def gate_vector(st, d, b, dz):
-            hh, u, th = st
-            nc.vector.scalar_tensor_tensor(
-                out=u[:], in0=hh[:], scalar=1.0, in1=u[:], op0=ALU.subtract, op1=ALU.mult
-            )
-            nc.vector.scalar_tensor_tensor(
-                out=u[:], in0=u[:], scalar=1.0, in1=d[:, :, 2 * b : 2 * b + 2, :], op0=ALU.subtract, op1=ALU.mult
-            )
-            for jj in range(2):
-                nc.vector.scalar_tensor_tensor(
-                    out=dz[:, 2 * b + jj, :].rearrange("p (h f) -> p h f", f=DV),
-                    in0=th[:, :, jj, :],
-                    scalar=1.0,
-                    in1=u[:, :, jj, :],
-                    op0=ALU.subtract,
-                    op1=ALU.mult,
-                )
-
-        def value_sums(cc, d, ss, s):
-            tv = cc[:].rearrange("p j (h e) -> p j h e", e=HD)
-            dv = d[:].rearrange("p h j f -> p j h f")
-            junk = tmp.tile([P, J * HH, DV], BF16, name="junk", tag="t")
-            for j in range(J):
-                for h in range(HH):
-                    i = HH * j + h
-                    nc.scalar.activation(
-                        out=junk[:, i, :], in_=tv[:, j, h, DK:HD], func=AF.Square, accum_out=ss[:, 64 + i : 65 + i]
-                    )
-            for q in range(2):
-                js = slice(2 * q, 2 * q + 2)
-                pr = tmp.tile([P, 2, HH, DV], F32, name="pv", tag="t")
-                nc.vector.tensor_tensor(out=pr[:], in0=tv[:, js, :, DK:HD], in1=dv[:, js], op=ALU.mult)
-                nc.vector.tensor_reduce(
-                    out=s[:, 64 + 16 * q : 80 + 16 * q],
-                    in_=pr[:].rearrange("p j h f -> p (j h) f"),
-                    axis=AX.X,
-                    op=ALU.add,
-                )
-
-        def value_finish(cc, d, r, c):
-            dz = dzp.tile([P, J, GT], BF16, name="dzv", tag="dz")
-            tv = cc[:].rearrange("p j (h e) -> p j h e", e=HD)
-            for q in range(2):
-                w = tmp.tile([P, 2, HH, DV], F32, name="wv", tag="t")
-                for jj in range(2):
-                    j = 2 * q + jj
-                    for h in range(HH):
-                        i = HH * j + h
-                        nc.scalar.activation(
-                            out=w[:, jj, h, :], in_=tv[:, j, h, DK:HD], func=AF.Copy, scale=c[:, 64 + i : 65 + i]
-                        )
-                        nc.vector.scalar_tensor_tensor(
-                            out=dz[:, j, DV * h : DV * (h + 1)],
-                            in0=d[:, h, j, :],
-                            scalar=r[:, 64 + i : 65 + i],
-                            in1=w[:, jj, h, :],
-                            op0=ALU.mult,
-                            op1=ALU.subtract,
-                        )
-            return dz
-
-        def rotate_back(g, d):
-            dp = rotp.tile([P, 2, H, J, DK], F32, name="dp")
-            nc.scalar.activation(
-                out=dp[:].rearrange("p s h j f -> p (s h j f)"),
-                in_=d[:].rearrange("p s h j f -> p (s h j f)"),
-                func=AF.Copy,
-            )
-            pair = d[:].rearrange("p s h j f -> p s (h j) f")[:, :, :, 0:2]
-            m = []
-            for c in range(2):
-                mc = rotp.tile([P, 2, H * J, 2], F32, name="m%d" % c)
-                tab = cs[:, c, g].rearrange("p (o h) (j t) -> p o (h j) t", o=1, t=1)
-                nc.vector.tensor_tensor(
-                    out=mc[:], in0=pair, in1=tab.to_broadcast([P, 2, H * J, 2]), op=ALU.mult
-                )
-                m.append(mc)
-            dst = dp[:].rearrange("p s h j f -> p s (h j) f")
-            nc.vector.tensor_tensor(
-                out=dst[:, :, :, 0], in0=m[0][:, :, :, 0], in1=m[1][:, :, :, 1], op=ALU.add
-            )
-            nc.vector.tensor_tensor(
-                out=dst[:, :, :, 1], in0=m[0][:, :, :, 1], in1=m[1][:, :, :, 0], op=ALU.subtract
-            )
-            return dp
-
-        def qk_sums(g, hf, a, cc, dp, ss, s_):
-            hs = slice(HH * hf, HH * (hf + 1))
-            sq = tmp.tile([P, 2, J, HH, DK], F32, name="qsq", tag="t")
-            pr = tmp.tile([P, 2, J, HH, DK], F32, name="qpr", tag="t")
-            tv, dv = [], []
-            for s, t in ((0, a), (1, cc)):
-                tv.append(t[:].rearrange("p j (h e) -> p j h e", e=HD)[:, :, :, 0:DK])
-                dv.append(dp[:, s, hs].rearrange("p h j f -> p j h f"))
-                nc.scalar.activation(out=sq[:, s], in_=tv[s], func=AF.Square)
-                nc.vector.tensor_tensor(out=pr[:, s], in0=tv[s], in1=dv[s], op=ALU.mult)
-            nc.vector.tensor_reduce(
-                out=ss[:, 0:64], in_=sq[:].rearrange("p s j h f -> p (s j h) f"), axis=AX.X, op=ALU.add
-            )
-            nc.vector.tensor_reduce(
-                out=s_[:, 0:64], in_=pr[:].rearrange("p s j h f -> p (s j h) f"), axis=AX.X, op=ALU.add
-            )
-            return tv, dv
-
-        def qk_finish(hf, tv, dv, r, c, dz0):
-            u = tmp.tile([P, 2, J, HH, DK], F32, name="qu", tag="t")
-            w = tmp.tile([P, 2, J, HH, DK], F32, name="qw", tag="t")
-            for s in range(2):
-                cols = slice(32 * s, 32 * s + 32)
-                nc.vector.tensor_tensor(out=u[:, s], in0=dv[s], in1=bcast(r[:, cols], DK), op=ALU.mult)
-                nc.vector.tensor_tensor(out=w[:, s], in0=tv[s], in1=bcast(c[:, cols], DK), op=ALU.mult)
-            nc.vector.tensor_tensor(
-                out=dz0[:].rearrange("p j (s c) -> p s j c", s=2)[:, :, :, 128 * hf : 128 * hf + 128],
-                in0=u[:].rearrange("p s j h f -> p s j (h f)"),
-                in1=w[:].rearrange("p s j h f -> p s j (h f)"),
-                op=ALU.subtract,
-            )
-
-        def token_quantise(g, which, hf, dz, dz0):
-            il = ilp.tile([P, HALF, J], BF16, name="il", tag="il", align_bytes=64)
-            rows = il[:].rearrange("p (h e) j -> p h e j", e=HD)
-            c0 = 256 * which + 128 * hf
-            nc.vector.tensor_copy(
-                out=rows[:, :, 0:DK, :], in_=dz0[:, :, c0 : c0 + 128].rearrange("p j (h f) -> p h f j", f=DK)
-            )
-            nc.vector.tensor_copy(out=rows[:, :, DK:HD, :], in_=dz[:].rearrange("p j (h f) -> p h f j", f=DV))
-            if g == 0:
-                codes = keep.tile([P, HALF], U32, name="dzc%d%d" % (which, hf), align_bytes=64)
-                scales = keep.tile([P, HALF], U8, name="dzs%d%d" % (which, hf), align_bytes=64)
+        def token_rows(k, which, part):
+            g, hf = UNITS[k]
+            if part == 0:
+                uil[(k, which)] = ilp.tile([P, HALF, J], BF16, name="il", tag="il", align_bytes=64)
+            rows = uil[(k, which)][:].rearrange("p (h e) j -> p h e j", e=HD)
+            if part == 0:
+                c0 = 256 * which + 128 * hf
+                src = udz0[g][:, :, c0 : c0 + 128].rearrange("p j (h f) -> p h f j", f=DK)
+                nc.vector.tensor_copy(out=rows[:, :, 0:DK, :], in_=src)
             else:
-                codes = ilp.tile([P, HALF], U32, name="dzc1", tag="dzc1", align_bytes=64)
-                scales = ilp.tile([P, HALF], U8, name="dzs1", tag="dzs1", align_bytes=64)
-            flat = il[:].rearrange("p n j -> p (n j)")
-            for lo, hi in ((0, 512), (512, 640)):
-                nc.vector.quantize_mx(
-                    out=codes[:, lo:hi].bitcast(E5M2), scales=scales[:, lo:hi], in_=flat[:, J * lo : J * hi]
-                )
-            dzc[(g, which, hf)] = (codes, scales)
+                src = (udzg, udzv)[which][k][:].rearrange("p j (h f) -> p h f j", f=DV)
+                nc.vector.tensor_copy(out=rows[:, :, DK:HD, :], in_=src)
+
+        def token_quantise(k, which, lo, hi):
+            g, hf = UNITS[k]
+            if lo == 0:
+                pool = keep if g == 0 else dzcp
+                key = "%d%d" % (which, hf) if g == 0 else ""
+                codes = pool.tile([P, HALF], U32, name="dzc" + key, align_bytes=64)
+                scales = pool.tile([P, HALF], U8, name="dzs" + key, align_bytes=64)
+                dzc[(g, which, hf)] = (codes, scales)
+            codes, scales = dzc[(g, which, hf)]
+            flat = uil[(k, which)][:].rearrange("p n j -> p (n j)")
+            nc.vector.quantize_mx(
+                out=codes[:, lo:hi].bitcast(E5M2), scales=scales[:, lo:hi], in_=flat[:, J * lo : J * hi]
+            )
+
+        def token_blocks(k, whichs=(0, 1)):
+            steps = [partial(token_rows, k, which, part) for which in whichs for part in range(2)]
+            return steps + [
+                partial(token_quantise, k, which, lo, hi) for which in whichs for lo, hi in ((0, 512), (512, HALF))
+            ]
 
         turn = [0]
+        wide = [False, 0]
+
+        def result_tile():
+            wide[1] += 1
+            if wide[0] and wide[1] % 2:
+                return ld.tile([P, DIM], F32, name="res", tag="ld")
+            return io.tile([P, DIM], F32, name="res", tag="io")
 
         def evacuate(out, acc, both):
             turn[0] += 1
@@ -376,10 +517,10 @@ def tile_gatedscreeningtile_pa_v_kernel(
             else:
                 nc.scalar.copy(out=out, in_=acc)
 
-        def weight_grad(which, hf, both=False):
+        def weight_rows(which, hf, m, both):
             dst = (out_1, out_2)[which]
-            for m in range(HALF // P):
-                res = outp.tile([P, DIM], F32, name="res", tag="res")
+            if True:
+                res = result_tile()
                 mc = slice(P * m, P * (m + 1))
                 for n in range(2):
                     cols = slice(512 * n, 512 * (n + 1))
@@ -399,7 +540,10 @@ def tile_gatedscreeningtile_pa_v_kernel(
                 r0 = HALF * hf + P * m
                 nc.sync.dma_start(out=dst[r0 : r0 + P, :], in_=res[:])
 
-        def token_grad_passes(g, j, n, acc, passes, first, last):
+        def weight_grad(which, hf, both=False):
+            return [partial(weight_rows, which, hf, m, both) for m in range(HALF // P)]
+
+        def token_passes(g, j, n, acc, passes, first, last):
             mc = slice(P * j, P * (j + 1))
             cols = slice(512 * n, 512 * (n + 1))
             for c in passes:
@@ -414,108 +558,133 @@ def tile_gatedscreeningtile_pa_v_kernel(
                     stop=(c == last),
                 )
 
-        def token_grad_open(g, js, passes):
-            opened = {}
+        opened = {}
+
+        def open_tokens(g, js, passes):
             for j in js:
                 for n in range(2):
                     acc = pacc.tile([P, 512], F32, name="accx", tag="acc")
-                    token_grad_passes(g, j, n, acc, passes, passes[0], None)
-                    opened[(j, n)] = acc
-            return opened
+                    token_passes(g, j, n, acc, passes, passes[0], None)
+                    opened[(g, j, n)] = acc
 
-        def token_grad(g, js, passes, opened, last, both=False):
+        def token_rows_grad(g, j, passes, both):
             rows = out_0[0, GT * g : GT * (g + 1), :].rearrange("(p j) w -> p j w", j=J)
-            for j in js:
-                res = outp.tile([P, DIM], F32, name="resx", tag="res")
+            if True:
+                res = result_tile()
                 for n in range(2):
-                    if (j, n) in opened:
-                        acc = opened[(j, n)]
-                        token_grad_passes(g, j, n, acc, [last], None, last)
+                    if (g, j, n) in opened:
+                        acc = opened[(g, j, n)]
+                        token_passes(g, j, n, acc, passes[-1:], None, passes[-1])
                     else:
                         acc = pacc.tile([P, 512], F32, name="accx", tag="acc")
-                        token_grad_passes(g, j, n, acc, passes + [last], passes[0], last)
+                        token_passes(g, j, n, acc, passes, passes[0], passes[-1])
                     evacuate(res[:, 512 * n : 512 * (n + 1)], acc[:], both)
                 nc.sync.dma_start(out=rows[:, j, :], in_=res[:])
 
-        qkds, dz0s, dps = {}, {}, {}
+        def token_grad(g, js, passes, both=False):
+            return [partial(token_rows_grad, g, j, passes, both) for j in js]
 
-        def load_unit(g, hf, a=None):
-            if a is None:
-                a = load_half(qg, g, hf)
-            cc = load_half(kv, g, hf)
-            d3 = load_grad(grad_3, g, hf)
-            if hf == 0:
-                qkds[g] = load_qk_grads(g)
-            d1 = load_grad(grad_1, g, hf)
-            return a, d1, cc, d3
+        prep_rot()
+        ua[0] = load_saved(qg, 0, 0)
+        raw_t0 = load_tokens(0, True)
+        ud1[0] = load_grad(grad_1, 0, 0)
+        uc[0] = load_saved(kv, 0, 0)
+        ud3[0] = load_grad(grad_3, 0, 0)
+        load_qk(0)
+        gate_scalar(0, 0)
+        load_raw(*order[0])
+        background = [partial(prepare, i, n) for i in range(len(order)) for n in range(2)]
+        g0 = group_on_vector(raw_t0, 0)
+        g1 = group_on_vector(raw_t0, 1)
+        quantise_piece(g0, t_codes[0], t_scales[0], 0)
+        quantise_piece(g1, t_codes[0], t_scales[0], 1)
+        load_unit(1)
+        gate_scalar(0, 1)
+        drain(gate_head(0, (0,)))
+        drain(gate_tail(0, (0,)))
+        squares(0)
+        cast_back(0)
+        v_products = products(0)
+        drain([v_products.pop(0), v_products.pop(0)])
+        drain(rotate_back(0))
+        drain(v_products)
 
-        def sums(g, hf, a, cc, d3):
-            ss = small.tile([P, 96], F32, name="ss")
-            s = small.tile([P, 96], F32, name="s")
-            tv, dv = qk_sums(g, hf, a, cc, dps[g], ss, s)
-            value_sums(cc, d3, ss, s)
-            r, c = norm_factors(ss, s, 96)
-            return tv, dv, r, c
+        def more(n=1):
+            for _ in range(n):
+                if background:
+                    background.pop(0)()
 
-        def unit(g, hf, a=None):
-            if hf == 0:
-                dz0s[g] = dzp.tile([P, J, GT], BF16, name="dz0", tag="dz0", bufs=1)
-            a, d1, cc, d3 = load_unit(g, hf, a)
-            if (g, hf) == (0, 0):
-                st = [gate_scalar(a, 0)]
-                prep_rot()
-            if hf == 0:
-                dps[g] = rotate_back(g, qkds[g])
-            tv, dv, r, c = sums(g, hf, a, cc, d3)
-            dzg = dzp.tile([P, J, GT], BF16, name="dzg", tag="dz")
-            if (g, hf) != (1, 1):
-                if (g, hf) != (0, 0):
-                    st = [gate_scalar(a, 0)]
-                st.append(gate_scalar(a, 1))
-                qk_finish(hf, tv, dv, r, c, dz0s[g])
-                dzv = value_finish(cc, d3, r, c)
-                for b in range(2):
-                    gate_vector(st[b], d1, b, dzg)
-                transpose_quantise(g, 3 + hf, dzv)
-                token_quantise(g, 1, hf, dzv, dz0s[g])
-                if g == 1:
-                    weight_grad(1, hf)
-                transpose_quantise(g, 1 + hf, dzg)
-                token_quantise(g, 0, hf, dzg, dz0s[g])
-                if g == 1:
-                    weight_grad(0, hf)
+        left = []
+        for k in range(4):
+            g, hf = UNITS[k]
+            gates = (0, 1) if k else (1,)
+            if k == 2:
+                background = token_grad(0, [0, 1, 2, 3], [0, 1, 2, 3, 4])
+            if k < 3:
+                left = gate_head(k, gates) + [settle] + gate_tail(k, gates) + [settle] + left
+                squares(k + 1)
+                weave(factors(k), left)
+                if k < 2:
+                    more()
+                transpose_features(g, 1 + hf, udzg[k])
+                gate_scalar(k + 1, 0)
+                if k < 2:
+                    more()
+                corrections(k)
+                drain(left)
+                settle()
+                finish(k)
+                settle()
+                cast_back(k + 1)
+                if k < 2:
+                    load_unit(k + 2)
+                more()
+                gate_scalar(k + 1, 1)
+                more()
+                drain(rotate_back(k + 1))
+                transpose_features(g, 3 + hf, udzv[k])
                 if hf == 1:
-                    transpose_quantise(g, 0, dz0s[g])
+                    transpose_features(g, 0, udz0[g])
+                products_next = products(k + 1)
+                for i in range(4):
+                    products_next.pop(0)()
+                drain(quantise_features(g, 1 + hf))
+                settle()
+                if k == 2:
+                    drain(token_blocks(k))
+                drain(products_next)
+                settle()
+                more(2)
+                left = quantise_features(g, 3 + hf)
+                if hf == 1:
+                    left = left + quantise_features(g, 0)
+                if k < 2:
+                    left = left + token_blocks(k)
             else:
-                st = [gate_scalar(a, 0)]
-                qk_finish(hf, tv, dv, r, c, dz0s[g])
-                dzv = value_finish(cc, d3, r, c)
-                transpose_quantise(g, 0, dz0s[g])
-                transpose_quantise(g, 4, dzv)
-                token_quantise(g, 1, hf, dzv, dz0s[g])
-                st.append(gate_scalar(a, 1))
-                weight_grad(1, hf)
-                gate_vector(st[0], d1, 0, dzg)
-                transpose_quantise(g, 2, dzg, (0,))
-                opened = token_grad_open(1, [0, 1], [0, 1, 3, 4])
-                gate_vector(st[1], d1, 1, dzg)
-                token_grad(1, [0, 1], None, opened, 2, True)
-                transpose_quantise(g, 2, dzg, (1,))
-                token_quantise(g, 0, hf, dzg, dz0s[g])
-                opened = token_grad_open(1, [2, 3], [0, 1, 3, 4])
-                token_grad(1, [2, 3], None, opened, 2, True)
-                weight_grad(0, hf, True)
-
-        a00 = load_half(qg, 0, 0)
-        prep_tokens(0)
-        unit(0, 0, a00)
-        prep_weights(1)
-        prep_weights(3)
-        unit(0, 1)
-        prep_weights(0)
-        prep_weights(2)
-        prep_weights(4)
-        prep_tokens(1)
-        token_grad(0, [0, 1, 2, 3], [0, 1, 2, 3], {}, 4)
-        unit(1, 0)
-        unit(1, 1)
+                drain(background)
+                background = weight_grad(0, 0) + weight_grad(1, 0)
+                left = left + gate_head(3, (0,))
+                weave(factors(k), left)
+                more(10)
+                wide[0] = True
+                corrections(k)
+                drain(left)
+                finish(k)
+                transpose_features(1, 4, udzv[3])
+                transpose_features(1, 0, udz0[1])
+                drain(token_blocks(3, (1,)))
+                drain(quantise_features(1, 4))
+                drain(quantise_features(1, 0))
+                drain(weight_grad(1, 1, False))
+                drain(gate_tail(3, (0,)))
+                drain(gate_head(3, (1,)))
+                open_tokens(1, [0, 1], [0, 1, 3, 4])
+                transpose_features(1, 2, udzg[3], (0,))
+                drain(gate_tail(3, (1,)))
+                drain(quantise_features(1, 2, (0,)))
+                transpose_features(1, 2, udzg[3], (1,))
+                drain(token_grad(1, [0, 1], [0, 1, 3, 4, 2], False))
+                drain(token_blocks(3, (0,)))
+                drain(quantise_features(1, 2, (1,)))
+                drain(token_grad(1, [2, 3], [0, 1, 3, 4, 2], True))
+                drain(weight_grad(0, 1, True))

@@ -46,7 +46,7 @@ def tile_gatedscreeningtile_pa_v_kernel(
         keep = ctx.enter_context(tc.tile_pool(name="keep", bufs=1))
         dztp = ctx.enter_context(tc.tile_pool(name="dztp", bufs=6))
         small = ctx.enter_context(tc.tile_pool(name="small", bufs=2))
-        rotp = ctx.enter_context(tc.tile_pool(name="rotp", bufs=1))
+        rotp = ctx.enter_context(tc.tile_pool(name="rotp", bufs=2))
         ptp = ctx.enter_context(tc.psum_pool(name="ptp", bufs=2))
         pacc = ctx.enter_context(tc.psum_pool(name="pacc", bufs=6))
         ctx.enter_context(tc.manual_schedule(engines={ENGINES.DVE, ENGINES.Activation, ENGINES.PE}))
@@ -54,7 +54,7 @@ def tile_gatedscreeningtile_pa_v_kernel(
         warm = const.tile([P, 1], F32, name="warm")
         nc.vector.memset(warm[:], 0.0)
         nc.scalar.activation(out=warm[:], in_=warm[:], func=AF.Silu)
-        junk = const.tile([P, HH, DV], BF16, name="junk")
+        junk = const.tile([P, DV], BF16, name="junk")
         ident = const.tile([P, P], F32, name="ident")
         make_identity(nc, ident[:])
         ident_b = const.tile([P, P], BF16, name="ident_b")
@@ -83,14 +83,13 @@ def tile_gatedscreeningtile_pa_v_kernel(
                 if filler:
                     filler.pop(0)()
 
-        def load_tokens(g, whole=False):
+        def load_token_columns(raw, g, n):
             rows = tokens[0, GT * g : GT * (g + 1), :].rearrange("(p j) w -> p j w", j=J)
-            if whole:
-                raw = ld.tile([P, J, DIM], BF16, name="raw_t0", tag="ld")
-                for n in range(2):
-                    cols = slice(512 * n, 512 * (n + 1))
-                    nc.sync.dma_start(out=raw[:, :, cols], in_=rows[:, :, cols])
-                return raw
+            cols = slice(512 * n, 512 * (n + 1))
+            nc.sync.dma_start(out=raw[:, :, cols], in_=rows[:, :, cols])
+
+        def load_tokens(g):
+            rows = tokens[0, GT * g : GT * (g + 1), :].rearrange("(p j) w -> p j w", j=J)
             raw = []
             for b in range(2):
                 raw.append(io.tile([P, 2, DIM], BF16, name="raw_t", tag="io"))
@@ -174,12 +173,15 @@ def tile_gatedscreeningtile_pa_v_kernel(
         usum, ufac, ugate, udzg, udzv, uw = {}, {}, {}, {}, {}, {}
         dzt, dzc = {}, {}
 
+        def load_slots(t, src, g, hf, b):
+            rows = src[0, GT * g : GT * (g + 1), :].rearrange("(p j) w -> p j w", j=J)
+            js = slice(2 * b, 2 * b + 2)
+            nc.sync.dma_start(out=t[:, js, :], in_=rows[:, js, HALF * hf : HALF * (hf + 1)])
+
         def load_saved(src, g, hf):
             t = ld.tile([P, J, HALF], F32, name="saved", tag="ld")
-            rows = src[0, GT * g : GT * (g + 1), :].rearrange("(p j) w -> p j w", j=J)
             for b in range(2):
-                js = slice(2 * b, 2 * b + 2)
-                nc.sync.dma_start(out=t[:, js, :], in_=rows[:, js, HALF * hf : HALF * (hf + 1)])
+                load_slots(t, src, g, hf, b)
             return t
 
         def load_grad(src, g, hf):
@@ -211,10 +213,13 @@ def tile_gatedscreeningtile_pa_v_kernel(
         def heads_of(t):
             return t[:].rearrange("p j (h e) -> p j h e", e=HD)
 
-        def prep_rot():
-            rt = tmp.tile([P, 2, GT], F32, name="rt", tag="t")
+        rt = tmp.tile([P, 2, GT], F32, name="rt", tag="t")
+
+        def load_rot():
             nc.vector.memset(rt[64:128, 0, :], 0.0)
             nc.sync.dma_start(out=rt[0:64, 0, :], in_=rot.rearrange("c h (g n) -> (c h g) n", g=2))
+
+        def spread_rot():
             rp = ptp.tile([P, J, P], F32, name="rp", tag="tp")
             for j in range(J):
                 nc.tensor.transpose(rp[:, j, :], rt[:, 0, j::J], ident[:])
@@ -241,7 +246,7 @@ def tile_gatedscreeningtile_pa_v_kernel(
             pair = uqk[g][:, :, hs].rearrange("p s h j f -> p s (h j) f")[:, :, :, 0:2]
             steps, m = [], []
             for c in range(2):
-                mc = small.tile([P, 2, HH * J, 2], F32, name="m%d" % c)
+                mc = small.tile([P, 2, HH * J, 2], F32, name="m%d" % c, bufs=1)
                 tab = cs[:, c, g, hs].rearrange("p (o h) (j t) -> p o (h j) t", o=1, t=1)
                 tab = tab.to_broadcast([P, 2, HH * J, 2])
                 steps.append(partial(nc.vector.tensor_tensor, out=mc[:], in0=pair, in1=tab, op=ALU.mult))
@@ -269,7 +274,7 @@ def tile_gatedscreeningtile_pa_v_kernel(
                 for h in range(HH):
                     i = 64 + HH * j + h
                     nc.scalar.activation(
-                        out=junk[:, h, :], in_=heads_of(uc[k])[:, j, h, DK:HD], func=AF.Square, accum_out=ss[:, i : i + 1]
+                        out=junk[:], in_=heads_of(uc[k])[:, j, h, DK:HD], func=AF.Square, accum_out=ss[:, i : i + 1]
                     )
             usum[k] = (ss, s, sq)
 
@@ -307,9 +312,9 @@ def tile_gatedscreeningtile_pa_v_kernel(
 
         def factors(k):
             ss, s, _ = usum[k]
-            x = small.tile([P, 96], F32, name="nx")
+            x = small.tile([P, 96], F32, name="nx", bufs=1)
             y = small.tile([P, 96], F32, name="ny")
-            z = small.tile([P, 96], F32, name="nz")
+            z = small.tile([P, 96], F32, name="nz", bufs=1)
             c = small.tile([P, 96], F32, name="nc_")
             ufac[k] = (y, c)
             yi = y[:].bitcast(I32)
@@ -563,9 +568,11 @@ def tile_gatedscreeningtile_pa_v_kernel(
         def open_tokens(g, js, passes):
             for j in js:
                 for n in range(2):
-                    acc = pacc.tile([P, 512], F32, name="accx", tag="acc")
-                    token_passes(g, j, n, acc, passes, passes[0], None)
-                    opened[(g, j, n)] = acc
+                    first = None
+                    if (g, j, n) not in opened:
+                        opened[(g, j, n)] = pacc.tile([P, 512], F32, name="accx", tag="acc")
+                        first = passes[0]
+                    token_passes(g, j, n, opened[(g, j, n)], passes, first, None)
 
         def token_rows_grad(g, j, passes, both):
             rows = out_0[0, GT * g : GT * (g + 1), :].rearrange("(p j) w -> p j w", j=J)
@@ -584,26 +591,31 @@ def tile_gatedscreeningtile_pa_v_kernel(
         def token_grad(g, js, passes, both=False):
             return [partial(token_rows_grad, g, j, passes, both) for j in js]
 
-        prep_rot()
-        ua[0] = load_saved(qg, 0, 0)
-        raw_t0 = load_tokens(0, True)
+        ua[0] = ld.tile([P, J, HALF], F32, name="saved", tag="ld")
+        load_slots(ua[0], qg, 0, 0, 0)
+        raw_t0 = ld.tile([P, J, DIM], BF16, name="raw_t0", tag="ld")
+        load_token_columns(raw_t0, 0, 0)
         ud1[0] = load_grad(grad_1, 0, 0)
+        load_token_columns(raw_t0, 0, 1)
+        load_slots(ua[0], qg, 0, 0, 1)
         uc[0] = load_saved(kv, 0, 0)
         ud3[0] = load_grad(grad_3, 0, 0)
+        load_rot()
         load_qk(0)
         gate_scalar(0, 0)
-        load_raw(*order[0])
         background = [partial(prepare, i, n) for i in range(len(order)) for n in range(2)]
         g0 = group_on_vector(raw_t0, 0)
         g1 = group_on_vector(raw_t0, 1)
         quantise_piece(g0, t_codes[0], t_scales[0], 0)
         quantise_piece(g1, t_codes[0], t_scales[0], 1)
         load_unit(1)
-        gate_scalar(0, 1)
+        load_raw(*order[0])
         drain(gate_head(0, (0,)))
-        drain(gate_tail(0, (0,)))
-        squares(0)
+        gate_scalar(0, 1)
+        spread_rot()
         cast_back(0)
+        squares(0)
+        drain(gate_tail(0, (0,)))
         v_products = products(0)
         drain([v_products.pop(0), v_products.pop(0)])
         drain(rotate_back(0))
@@ -619,23 +631,29 @@ def tile_gatedscreeningtile_pa_v_kernel(
             g, hf = UNITS[k]
             gates = (0, 1) if k else (1,)
             if k == 2:
-                background = token_grad(0, [0, 1, 2, 3], [0, 1, 2, 3, 4])
+                background = background + token_grad(0, [0, 1, 2, 3], [0, 1, 2, 3, 4])
             if k < 3:
                 left = gate_head(k, gates) + [settle] + gate_tail(k, gates) + [settle] + left
                 squares(k + 1)
+                if hf == 0:
+                    cast_back(k + 1)
                 weave(factors(k), left)
-                if k < 2:
+                if k > 0 and k < 3:
                     more()
                 transpose_features(g, 1 + hf, udzg[k])
+                if k == 0:
+                    corrections(k)
                 gate_scalar(k + 1, 0)
-                if k < 2:
+                if k == 1:
                     more()
-                corrections(k)
+                if k > 0:
+                    corrections(k)
                 drain(left)
                 settle()
                 finish(k)
                 settle()
-                cast_back(k + 1)
+                if hf == 1:
+                    cast_back(k + 1)
                 if k < 2:
                     load_unit(k + 2)
                 more()
@@ -667,6 +685,7 @@ def tile_gatedscreeningtile_pa_v_kernel(
                 weave(factors(k), left)
                 more(10)
                 wide[0] = True
+                open_tokens(1, [0, 1], [1, 3])
                 corrections(k)
                 drain(left)
                 finish(k)
@@ -675,15 +694,17 @@ def tile_gatedscreeningtile_pa_v_kernel(
                 drain(token_blocks(3, (1,)))
                 drain(quantise_features(1, 4))
                 drain(quantise_features(1, 0))
-                drain(weight_grad(1, 1, False))
                 drain(gate_tail(3, (0,)))
                 drain(gate_head(3, (1,)))
-                open_tokens(1, [0, 1], [0, 1, 3, 4])
+                last = weight_grad(1, 1, False)
+                drain(last[0:3])
                 transpose_features(1, 2, udzg[3], (0,))
+                drain(last[3:5])
                 drain(gate_tail(3, (1,)))
                 drain(quantise_features(1, 2, (0,)))
+                open_tokens(1, [0, 1], [0, 4])
                 transpose_features(1, 2, udzg[3], (1,))
-                drain(token_grad(1, [0, 1], [0, 1, 3, 4, 2], False))
+                drain(token_grad(1, [0, 1], [1, 3, 0, 4, 2], False))
                 drain(token_blocks(3, (0,)))
                 drain(quantise_features(1, 2, (1,)))
                 drain(token_grad(1, [2, 3], [0, 1, 3, 4, 2], True))

@@ -26,6 +26,7 @@ J = 4
 GT = 512
 HH = 8
 HALF = HH * HD
+HEAD_GROUPS = ((0, 6), (6, 8))
 UNITS = ((0, 0), (0, 1), (1, 0), (1, 1))
 
 
@@ -54,15 +55,17 @@ def tile_gatedscreeningtile_pa_v_kernel(
         warm = const.tile([P, 1], F32, name="warm")
         nc.vector.memset(warm[:], 0.0)
         nc.scalar.activation(out=warm[:], in_=warm[:], func=AF.Silu)
-        junk = const.tile([P, DV], BF16, name="junk")
         ident = const.tile([P, P], F32, name="ident")
         make_identity(nc, ident[:])
         ident_b = const.tile([P, P], BF16, name="ident_b")
         make_identity(nc, ident_b[:])
         perm_b = const.tile([P, P], BF16, name="perm_b")
-        nc.vector.tensor_copy(
-            out=perm_b[:].rearrange("p (h d) -> p h d", h=HH), in_=ident_b[:].rearrange("p (d h) -> p h d", h=HH)
-        )
+        for h0, h1 in HEAD_GROUPS:
+            cols = slice(16 * h0, 16 * h1)
+            nc.vector.tensor_copy(
+                out=perm_b[:, cols].rearrange("p (h d) -> p h d", h=h1 - h0),
+                in_=ident_b[:, cols].rearrange("p (d h) -> p h d", h=h1 - h0),
+            )
         cs = const.tile([P, 2, 2, H, J], F32, name="cs")
 
         t_codes, t_scales, w_codes, w_scales = [], [], [], []
@@ -113,10 +116,9 @@ def tile_gatedscreeningtile_pa_v_kernel(
                     w = w_qg if c < 3 else w_kv
                     h0 = HH * ((c - 1) % 2)
                     heads = w[HD * h0 : HD * (h0 + HH), :].rearrange("(h e) w -> h e w", e=HD)[:, DK:HD, :]
-                    nc.sync.dma_start(
-                        out=flat,
-                        in_=heads.rearrange("h (p j) w -> p h j w", j=J)[:, :, js, :].rearrange("p h j w -> p h (j w)"),
-                    )
+                    rows = heads.rearrange("h (p j) w -> p h j w", j=J)[:, :, js, :].rearrange("p h j w -> p h (j w)")
+                    for lo, hi in HEAD_GROUPS:
+                        nc.sync.dma_start(out=flat[16 * lo : 16 * hi, :], in_=rows[:, lo:hi, :])
             return raw
 
         def quantise_piece(grouped, codes, scales, n):
@@ -268,13 +270,14 @@ def tile_gatedscreeningtile_pa_v_kernel(
             ss = small.tile([P, 96], F32, name="ss")
             s = small.tile([P, 96], F32, name="s")
             sq = tmp.tile([P, 2, J, HH, DK], F32, name="qsq", tag="t")
+            junk = tmp.tile([P, J, HH, DV], BF16, name="junk", tag="t")
             for i, t in enumerate((ua[k], uc[k])):
                 nc.scalar.activation(out=sq[:, i], in_=heads_of(t)[:, :, :, 0:DK], func=AF.Square)
             for j in range(J):
                 for h in range(HH):
                     i = 64 + HH * j + h
                     nc.scalar.activation(
-                        out=junk[:], in_=heads_of(uc[k])[:, j, h, DK:HD], func=AF.Square, accum_out=ss[:, i : i + 1]
+                        out=junk[:, j, h, :], in_=heads_of(uc[k])[:, j, h, DK:HD], func=AF.Square, accum_out=ss[:, i : i + 1]
                     )
             usum[k] = (ss, s, sq)
 
@@ -305,7 +308,7 @@ def tile_gatedscreeningtile_pa_v_kernel(
                     )
                 )
             sums.append((pr[:].rearrange("p s j h f -> p (s j h) f"), s[:, 0:64]))
-            sums.append((sq[:].rearrange("p s j h f -> p (s j h) f"), ss[:, 0:64]))
+            sums = [(sq[:].rearrange("p s j h f -> p (s j h) f"), ss[:, 0:64])] + sums
             for src, dst in sums:
                 steps.append(partial(nc.vector.tensor_reduce, out=dst, in_=src, axis=AX.X, op=ALU.add))
             return steps
@@ -321,8 +324,9 @@ def tile_gatedscreeningtile_pa_v_kernel(
             ts, tt, stt = nc.vector.tensor_scalar, nc.vector.tensor_tensor, nc.vector.scalar_tensor_tensor
             steps = [
                 partial(ts, out=x[:], in0=ss[:], scalar1=1e-24, scalar2=None, op0=ALU.max),
-                partial(ts, out=yi, in0=x[:].bitcast(I32), scalar1=1, scalar2=None, op0=ALU.arith_shift_right),
-                partial(ts, out=yi, in0=yi, scalar1=-1.0, scalar2=1597463007.0, op0=ALU.mult, op1=ALU.add),
+                partial(
+                    ts, out=yi, in0=x[:].bitcast(I32), scalar1=-0.5, scalar2=1597463007.0, op0=ALU.mult, op1=ALU.add
+                ),
             ]
             for it in range(3):
                 steps += [
@@ -592,8 +596,8 @@ def tile_gatedscreeningtile_pa_v_kernel(
             return [partial(token_rows_grad, g, j, passes, both) for j in js]
 
         ua[0] = ld.tile([P, J, HALF], F32, name="saved", tag="ld")
-        load_slots(ua[0], qg, 0, 0, 0)
         raw_t0 = ld.tile([P, J, DIM], BF16, name="raw_t0", tag="ld")
+        load_slots(ua[0], qg, 0, 0, 0)
         load_token_columns(raw_t0, 0, 0)
         ud1[0] = load_grad(grad_1, 0, 0)
         load_token_columns(raw_t0, 0, 1)
@@ -602,14 +606,14 @@ def tile_gatedscreeningtile_pa_v_kernel(
         ud3[0] = load_grad(grad_3, 0, 0)
         load_rot()
         load_qk(0)
-        gate_scalar(0, 0)
+        load_unit(1)
+        load_raw(*order[0])
         background = [partial(prepare, i, n) for i in range(len(order)) for n in range(2)]
+        gate_scalar(0, 0)
         g0 = group_on_vector(raw_t0, 0)
         g1 = group_on_vector(raw_t0, 1)
         quantise_piece(g0, t_codes[0], t_scales[0], 0)
         quantise_piece(g1, t_codes[0], t_scales[0], 1)
-        load_unit(1)
-        load_raw(*order[0])
         drain(gate_head(0, (0,)))
         gate_scalar(0, 1)
         spread_rot()
@@ -669,25 +673,26 @@ def tile_gatedscreeningtile_pa_v_kernel(
                 drain(quantise_features(g, 1 + hf))
                 settle()
                 if k == 2:
-                    drain(token_blocks(k))
+                    drain(token_blocks(k, (0,)))
                 drain(products_next)
                 settle()
                 more(2)
                 left = quantise_features(g, 3 + hf)
                 if hf == 1:
                     left = left + quantise_features(g, 0)
-                if k < 2:
-                    left = left + token_blocks(k)
+                left = left + token_blocks(k, (0, 1) if k < 2 else (1,))
             else:
                 drain(background)
                 background = weight_grad(0, 0) + weight_grad(1, 0)
+                more(4)
                 left = left + gate_head(3, (0,))
                 weave(factors(k), left)
-                more(10)
+                drain(left)
+                more(4)
+                corrections(k)
+                more(2)
                 wide[0] = True
                 open_tokens(1, [0, 1], [1, 3])
-                corrections(k)
-                drain(left)
                 finish(k)
                 transpose_features(1, 4, udzv[3])
                 transpose_features(1, 0, udz0[1])
@@ -707,5 +712,5 @@ def tile_gatedscreeningtile_pa_v_kernel(
                 drain(token_grad(1, [0, 1], [1, 3, 0, 4, 2], False))
                 drain(token_blocks(3, (0,)))
                 drain(quantise_features(1, 2, (1,)))
-                drain(token_grad(1, [2, 3], [0, 1, 3, 4, 2], True))
+                drain(token_grad(1, [2, 3], [1, 3, 0, 4, 2], True))
                 drain(weight_grad(0, 1, True))

from contextlib import ExitStack
from functools import partial

import concourse.mybir as mybir
from concourse.masks import make_identity

N, DIM, H, DK, DV = 1024, 1024, 16, 16, 64
HD = DK + DV
DI = H * HD
FLOPS = 2 * 2 * N * (2 * DI) * DIM

F32 = mybir.dt.float32
BF16 = mybir.dt.bfloat16
I32 = mybir.dt.int32
U32 = mybir.dt.uint32
U8 = mybir.dt.uint8
E4M3 = mybir.dt.float8_e4m3fn_x4
E5M2 = mybir.dt.float8_e5m2_x4
AF = mybir.ActivationFunctionType
ALU = mybir.AluOpType
AX = mybir.AxisListType
ENGINES = mybir.EngineType

P = 128
J = 4
GT = 512
HH = 8
HALF = HH * HD
HEAD_GROUPS = ((0, 6), (6, 8))
UNITS = ((0, 0), (0, 1), (1, 0), (1, 1))


def tile_gatedscreeningtile_pa_v_kernel(
    tc, tokens, w_qg, w_kv, sm_log, qg, kv, rot, grad_0, grad_1, grad_2, grad_3, out_0, out_1, out_2
):
    nc = tc.nc
    with ExitStack() as ctx:
        const = ctx.enter_context(tc.tile_pool(name="const", bufs=1))
        ld = ctx.enter_context(tc.tile_pool(name="ld", bufs=4))
        io = ctx.enter_context(tc.tile_pool(name="io", bufs=4))
        gr = ctx.enter_context(tc.tile_pool(name="gr", bufs=5))
        tmp = ctx.enter_context(tc.tile_pool(name="tmp", bufs=10))
        dzp = ctx.enter_context(tc.tile_pool(name="dzp", bufs=3))
        ilp = ctx.enter_context(tc.tile_pool(name="ilp", bufs=3))
        grp = ctx.enter_context(tc.tile_pool(name="grp", bufs=2))
        dzcp = ctx.enter_context(tc.tile_pool(name="dzcp", bufs=2))
        keep = ctx.enter_context(tc.tile_pool(name="keep", bufs=1))
        dztp = ctx.enter_context(tc.tile_pool(name="dztp", bufs=6))
        small = ctx.enter_context(tc.tile_pool(name="small", bufs=2))
        rotp = ctx.enter_context(tc.tile_pool(name="rotp", bufs=2))
        ptp = ctx.enter_context(tc.psum_pool(name="ptp", bufs=2))
        pacc = ctx.enter_context(tc.psum_pool(name="pacc", bufs=6))
        ctx.enter_context(tc.manual_schedule(engines={ENGINES.DVE, ENGINES.Activation, ENGINES.PE}))

        warm = const.tile([P, 1], F32, name="warm")
        nc.vector.memset(warm[:], 0.0)
        nc.scalar.activation(out=warm[:], in_=warm[:], func=AF.Silu)
        ident = const.tile([P, P], F32, name="ident")
        make_identity(nc, ident[:])
        ident_b = const.tile([P, P], BF16, name="ident_b")
        make_identity(nc, ident_b[:])
        perm_b = const.tile([P, P], BF16, name="perm_b")
        for h0, h1 in HEAD_GROUPS:
            cols = slice(16 * h0, 16 * h1)
            nc.vector.tensor_copy(
                out=perm_b[:, cols].rearrange("p (h d) -> p h d", h=h1 - h0),
                in_=ident_b[:, cols].rearrange("p (d h) -> p h d", h=h1 - h0),
            )
        cs = const.tile([P, 2, 2, H, J], F32, name="cs")

        t_codes, t_scales, w_codes, w_scales = [], [], [], []
        for g in range(2):
            t_codes.append(keep.tile([P, DIM], U32, name="t_codes%d" % g, align_bytes=64))
            t_scales.append(keep.tile([P, DIM], U8, name="t_scales%d" % g, align_bytes=64))
        for c in range(5):
            w_codes.append(keep.tile([P, DIM], U32, name="w_codes%d" % c, align_bytes=64))
            w_scales.append(keep.tile([P, DIM], U8, name="w_scales%d" % c, align_bytes=64))

        def drain(steps):
            while steps:
                steps.pop(0)()

        def weave(main, filler):
            for step in main:
                step()
                if filler:
                    filler.pop(0)()

        def load_token_columns(raw, g, n):
            rows = tokens[0, GT * g : GT * (g + 1), :].rearrange("(p j) w -> p j w", j=J)
            cols = slice(512 * n, 512 * (n + 1))
            nc.sync.dma_start(out=raw[:, :, cols], in_=rows[:, :, cols])

        def load_tokens(g):
            rows = tokens[0, GT * g : GT * (g + 1), :].rearrange("(p j) w -> p j w", j=J)
            raw = []
            for b in range(2):
                raw.append(io.tile([P, 2, DIM], BF16, name="raw_t", tag="io"))
                nc.sync.dma_start(out=raw[b][:], in_=rows[:, 2 * b : 2 * b + 2, :])
            return raw

        def load_weights(c):
            raw = []
            for b in range(2):
                raw.append(io.tile([P, 2, DIM], BF16, name="raw_w", tag="io"))
                flat = raw[b][:].rearrange("p j w -> p (j w)")
                js = slice(2 * b, 2 * b + 2)
                if c == 0:
                    for s, w in ((0, w_qg), (1, w_kv)):
                        heads = w.rearrange("(h e) w -> h e w", e=HD)[:, 0:DK, :]
                        nc.sync.dma_start(
                            out=flat[64 * s : 64 * s + 64, :],
                            in_=heads.rearrange("h (p j) w -> h p j w", j=J)[:, :, js, :].rearrange("h p j w -> h p (j w)"),
                        )
                else:
                    w = w_qg if c < 3 else w_kv
                    h0 = HH * ((c - 1) % 2)
                    heads = w[HD * h0 : HD * (h0 + HH), :].rearrange("(h e) w -> h e w", e=HD)[:, DK:HD, :]
                    rows = heads.rearrange("h (p j) w -> p h j w", j=J)[:, :, js, :].rearrange("p h j w -> p h (j w)")
                    for lo, hi in HEAD_GROUPS:
                        nc.sync.dma_start(out=flat[16 * lo : 16 * hi, :], in_=rows[:, lo:hi, :])
            return raw

        def quantise_piece(grouped, codes, scales, n):
            cols = slice(512 * n, 512 * (n + 1))
            nc.vector.quantize_mx(
                out=codes[:, cols].bitcast(E4M3),
                scales=scales[:, cols],
                in_=grouped[:, 0:512, :].rearrange("p w j -> p (w j)"),
            )

        def group_on_vector(raw, n):
            grouped = ilp.tile([P, HALF, J], BF16, name="grouped_v", tag="il", align_bytes=64)
            nc.vector.tensor_copy(
                out=grouped[:, 0:512, :], in_=raw[:, :, 512 * n : 512 * (n + 1)].rearrange("p j w -> p w j")
            )
            return grouped

        def group_on_tensor(raw, n, mover):
            grouped = grp.tile([P, 512, J], BF16, name="grouped_t", tag="grp", align_bytes=64)
            for k in range(2):
                mv = pacc.tile([P, 256, J], BF16, name="mv", tag="acc")
                c0 = 512 * n + 256 * k
                for b in range(2):
                    nc.tensor.matmul(
                        mv[:, :, 2 * b : 2 * b + 2],
                        lhsT=mover[:],
                        rhs=raw[b][:, :, c0 : c0 + 256].rearrange("p j w -> p w j"),
                        start=True,
                        stop=True,
                    )
                nc.scalar.copy(out=grouped[:, 256 * k : 256 * (k + 1), :], in_=mv[:])
            return grouped

        order = [("w", 1), ("w", 2), ("w", 3), ("w", 4), ("w", 0), ("t", 1)]
        raws = {}
        pending = []

        def load_raw(kind, c):
            raws[(kind, c)] = load_weights(c) if kind == "w" else load_tokens(c)

        def prepare(i, n):
            kind, c = order[i]
            if n == 0 and i + 1 < len(order):
                load_raw(*order[i + 1])
            codes, scales = (w_codes[c], w_scales[c]) if kind == "w" else (t_codes[c], t_scales[c])
            mover = perm_b if kind == "w" and c > 0 else ident_b
            pending.append((group_on_tensor(raws[(kind, c)], n, mover), codes, scales, n))

        def settle():
            if pending:
                quantise_piece(*pending.pop(0))

        ua, uc, ud1, ud3, uqk, urot, udz0 = {}, {}, {}, {}, {}, {}, {}
        usum, ufac, ugate, udzg, udzv, uw = {}, {}, {}, {}, {}, {}
        dzt, dzc = {}, {}

        def load_slots(t, src, g, hf, b):
            rows = src[0, GT * g : GT * (g + 1), :].rearrange("(p j) w -> p j w", j=J)
            js = slice(2 * b, 2 * b + 2)
            nc.sync.dma_start(out=t[:, js, :], in_=rows[:, js, HALF * hf : HALF * (hf + 1)])

        def load_saved(src, g, hf):
            t = ld.tile([P, J, HALF], F32, name="saved", tag="ld")
            for b in range(2):
                load_slots(t, src, g, hf, b)
            return t

        def load_grad(src, g, hf):
            t = gr.tile([P, HH, J, DV], BF16, name="grad", tag="gr")
            nc.sync.dma_start(
                out=t[:].rearrange("p h j f -> p h (j f)"),
                in_=src[0, HH * hf : HH * (hf + 1), GT * g : GT * (g + 1), :].rearrange("h (p j) f -> p h (j f)", j=J),
            )
            return t

        def load_qk(g):
            t = gr.tile([P, 2, H, J, DK], BF16, name="qkgrad", tag="gr")
            for s, src in ((0, grad_0), (1, grad_2)):
                nc.sync.dma_start(
                    out=t[:, s].rearrange("p h j f -> p h (j f)"),
                    in_=src[0, :, GT * g : GT * (g + 1), :].rearrange("h (p j) f -> p h (j f)", j=J),
                )
            uqk[g] = t

        def load_unit(k):
            g, hf = UNITS[k]
            ua[k] = load_saved(qg, g, hf)
            uc[k] = load_saved(kv, g, hf)
            ud3[k] = load_grad(grad_3, g, hf)
            if hf == 0:
                load_qk(g)
            ud1[k] = load_grad(grad_1, g, hf)

        def heads_of(t):
            return t[:].rearrange("p j (h e) -> p j h e", e=HD)

        rt = tmp.tile([P, 2, GT], F32, name="rt", tag="t")

        def load_rot():
            nc.vector.memset(rt[64:128, 0, :], 0.0)
            nc.sync.dma_start(out=rt[0:64, 0, :], in_=rot.rearrange("c h (g n) -> (c h g) n", g=2))

        def spread_rot():
            rp = ptp.tile([P, J, P], F32, name="rp", tag="tp")
            for j in range(J):
                nc.tensor.transpose(rp[:, j, :], rt[:, 0, j::J], ident[:])
            for c in range(2):
                for g in range(2):
                    nc.scalar.copy(
                        out=cs[:, c, g, :, :],
                        in_=rp[:, :, 32 * c : 32 * c + 32].rearrange("p j (h g) -> p g h j", g=2)[:, g, :, :],
                    )

        def cast_back(k):
            g, hf = UNITS[k]
            dp = rotp.tile([P, 2, HH, J, DK], F32, name="dp")
            nc.scalar.activation(
                out=dp[:].rearrange("p s h j f -> p s (h j f)"),
                in_=uqk[g][:, :, HH * hf : HH * (hf + 1)].rearrange("p s h j f -> p s (h j f)"),
                func=AF.Copy,
            )
            urot[k] = dp

        def rotate_back(k):
            g, hf = UNITS[k]
            hs = slice(HH * hf, HH * (hf + 1))
            pair = uqk[g][:, :, hs].rearrange("p s h j f -> p s (h j) f")[:, :, :, 0:2]
            steps, m = [], []
            for c in range(2):
                mc = small.tile([P, 2, HH * J, 2], F32, name="m%d" % c, bufs=1)
                tab = cs[:, c, g, hs].rearrange("p (o h) (j t) -> p o (h j) t", o=1, t=1)
                tab = tab.to_broadcast([P, 2, HH * J, 2])
                steps.append(partial(nc.vector.tensor_tensor, out=mc[:], in0=pair, in1=tab, op=ALU.mult))
                m.append(mc)
            dst = urot[k][:].rearrange("p s h j f -> p s (h j) f")
            for i, op in ((0, ALU.add), (1, ALU.subtract)):
                steps.append(
                    partial(
                        nc.vector.tensor_tensor,
                        out=dst[:, :, :, i],
                        in0=m[0][:, :, :, i],
                        in1=m[1][:, :, :, 1 - i],
                        op=op,
                    )
                )
            return steps

        def squares(k):
            ss = small.tile([P, 96], F32, name="ss")
            s = small.tile([P, 96], F32, name="s")
            sq = tmp.tile([P, 2, J, HH, DK], F32, name="qsq", tag="t")
            junk = tmp.tile([P, J, HH, DV], BF16, name="junk", tag="t")
            for i, t in enumerate((ua[k], uc[k])):
                nc.scalar.activation(out=sq[:, i], in_=heads_of(t)[:, :, :, 0:DK], func=AF.Square)
            for j in range(J):
                for h in range(HH):
                    i = 64 + HH * j + h
                    nc.scalar.activation(
                        out=junk[:, j, h, :], in_=heads_of(uc[k])[:, j, h, DK:HD], func=AF.Square, accum_out=ss[:, i : i + 1]
                    )
            usum[k] = (ss, s, sq)

        def rotated(k, s):
            return urot[k][:, s].rearrange("p h j f -> p j h f")

        def products(k):
            ss, s, sq = usum[k]
            dv = ud3[k][:].rearrange("p h j f -> p j h f")
            tv = heads_of(uc[k])
            pr = tmp.tile([P, 2, J, HH, DK], F32, name="qpr", tag="t")
            steps, sums = [], []
            for i in range(2):
                js = slice(2 * i, 2 * i + 2)
                pv = tmp.tile([P, 2, HH, DV], F32, name="pv", tag="t")
                steps.append(
                    partial(nc.vector.tensor_tensor, out=pv[:], in0=tv[:, js, :, DK:HD], in1=dv[:, js], op=ALU.mult)
                )
                sums.append((pv[:].rearrange("p j h f -> p (j h) f"), s[:, 64 + 16 * i : 80 + 16 * i]))
            for i, t in enumerate((ua[k], uc[k])):
                steps.append(
                    partial(
                        nc.vector.tensor_tensor,
                        out=pr[:, i],
                        in0=heads_of(t)[:, :, :, 0:DK],
                        in1=rotated(k, i),
                        op=ALU.mult,
                    )
                )
            sums.append((pr[:].rearrange("p s j h f -> p (s j h) f"), s[:, 0:64]))
            sums = [(sq[:].rearrange("p s j h f -> p (s j h) f"), ss[:, 0:64])] + sums
            for src, dst in sums:
                steps.append(partial(nc.vector.tensor_reduce, out=dst, in_=src, axis=AX.X, op=ALU.add))
            return steps

        def factors(k):
            ss, s, _ = usum[k]
            x = small.tile([P, 96], F32, name="nx", bufs=1)
            y = small.tile([P, 96], F32, name="ny")
            z = small.tile([P, 96], F32, name="nz", bufs=1)
            c = small.tile([P, 96], F32, name="nc_")
            ufac[k] = (y, c)
            yi = y[:].bitcast(I32)
            ts, tt, stt = nc.vector.tensor_scalar, nc.vector.tensor_tensor, nc.vector.scalar_tensor_tensor
            steps = [
                partial(ts, out=x[:], in0=ss[:], scalar1=1e-24, scalar2=None, op0=ALU.max),
                partial(
                    ts, out=yi, in0=x[:].bitcast(I32), scalar1=-0.5, scalar2=1597463007.0, op0=ALU.mult, op1=ALU.add
                ),
            ]
            for it in range(3):
                steps += [
                    partial(tt, out=z[:], in0=y[:], in1=y[:], op=ALU.mult),
                    partial(stt, out=z[:], in0=z[:], scalar=-0.5, in1=x[:], op0=ALU.mult, op1=ALU.mult),
                    partial(stt, out=y[:], in0=z[:], scalar=1.5, in1=y[:], op0=ALU.add, op1=ALU.mult),
                ]
            steps += [
                partial(tt, out=z[:], in0=y[:], in1=y[:], op=ALU.mult),
                partial(tt, out=c[:], in0=y[:], in1=s[:], op=ALU.mult),
                partial(tt, out=c[:], in0=c[:], in1=z[:], op=ALU.mult),
            ]
            return steps

        def corrections(k):
            _, c = ufac[k]
            uw[k] = []
            for q in range(2):
                w = tmp.tile([P, 2, HH, DV], F32, name="wv", tag="t")
                uw[k].append(w)
                for jj in range(2):
                    for h in range(HH):
                        i = 64 + HH * (2 * q + jj) + h
                        nc.scalar.activation(
                            out=w[:, jj, h, :],
                            in_=heads_of(uc[k])[:, 2 * q + jj, h, DK:HD],
                            func=AF.Copy,
                            scale=c[:, i : i + 1],
                        )

        def bcast(ap):
            return ap.rearrange("p (j h o) -> p j h o", h=HH, o=1).to_broadcast([P, J, HH, DK])

        def finish_qk(k):
            y, c = ufac[k]
            qu = tmp.tile([P, 2, J, HH, DK], F32, name="qu", tag="t")
            qw = tmp.tile([P, 2, J, HH, DK], F32, name="qw", tag="t")
            for s, t in enumerate((ua[k], uc[k])):
                cols = slice(32 * s, 32 * s + 32)
                nc.vector.tensor_tensor(out=qu[:, s], in0=rotated(k, s), in1=bcast(y[:, cols]), op=ALU.mult)
                nc.vector.tensor_tensor(
                    out=qw[:, s], in0=heads_of(t)[:, :, :, 0:DK], in1=bcast(c[:, cols]), op=ALU.mult
                )
            return qu, qw

        def finish_v(k, q):
            y, _ = ufac[k]
            for jj in range(2):
                j = 2 * q + jj
                for h in range(HH):
                    i = 64 + HH * j + h
                    nc.vector.scalar_tensor_tensor(
                        out=udzv[k][:, j, DV * h : DV * (h + 1)],
                        in0=ud3[k][:, h, j, :],
                        scalar=y[:, i : i + 1],
                        in1=uw[k][q][:, jj, h, :],
                        op0=ALU.mult,
                        op1=ALU.subtract,
                    )

        def finish(k):
            g, hf = UNITS[k]
            if hf == 0:
                udz0[g] = dzp.tile([P, J, GT], BF16, name="dz0", tag="dz0", bufs=1)
            qu, qw = finish_qk(k)
            udzv[k] = dzp.tile([P, J, GT], BF16, name="dzv", tag="dz")
            finish_v(k, 0)
            nc.vector.tensor_tensor(
                out=udz0[g][:].rearrange("p j (s c) -> p s j c", s=2)[:, :, :, 128 * hf : 128 * hf + 128],
                in0=qu[:].rearrange("p s j h f -> p s j (h f)"),
                in1=qw[:].rearrange("p s j h f -> p s j (h f)"),
                op=ALU.subtract,
            )
            finish_v(k, 1)

        def gate_scalar(k, b):
            gv = ua[k][:].rearrange("p j (h e) -> p h j e", e=HD)[:, :, 2 * b : 2 * b + 2, DK:HD]
            u = tmp.tile([P, HH, 2, DV], F32, name="gu", tag="t")
            nc.scalar.activation(out=u[:], in_=gv, func=AF.Silu)
            hh = tmp.tile([P, HH, 2, DV], F32, name="gh", tag="t")
            nc.scalar.activation(out=hh[:], in_=gv, func=AF.Tanh, scale=0.5)
            th = tmp.tile([P, HH, 2, DV], F32, name="gth", tag="t")
            nc.scalar.activation(out=th[:], in_=u[:], func=AF.Tanh)
            nc.scalar.activation(out=u[:], in_=u[:], func=AF.Copy, scale=0.5, bias=-0.5)
            nc.scalar.activation(out=th[:], in_=th[:], func=AF.Square)
            ugate[(k, b)] = (hh, u, th)

        def gate_m(k, b):
            hh, u, _ = ugate[(k, b)]
            nc.vector.scalar_tensor_tensor(out=u[:], in0=hh[:], scalar=1.0, in1=u[:], op0=ALU.subtract, op1=ALU.mult)

        def gate_k(k, b):
            _, u, _ = ugate[(k, b)]
            d = ud1[k][:, :, 2 * b : 2 * b + 2, :]
            nc.vector.scalar_tensor_tensor(out=u[:], in0=u[:], scalar=1.0, in1=d, op0=ALU.subtract, op1=ALU.mult)

        def gate_dz(k, b, jj):
            if k not in udzg:
                udzg[k] = dzp.tile([P, J, GT], BF16, name="dzg", tag="dz")
            _, u, th = ugate[(k, b)]
            nc.vector.scalar_tensor_tensor(
                out=udzg[k][:, 2 * b + jj, :].rearrange("p (h f) -> p h f", f=DV),
                in0=th[:, :, jj, :],
                scalar=1.0,
                in1=u[:, :, jj, :],
                op0=ALU.subtract,
                op1=ALU.mult,
            )

        def gate_head(k, bs):
            return [partial(gate_m, k, b) for b in bs] + [partial(gate_k, k, b) for b in bs]

        def gate_tail(k, bs):
            return [partial(gate_dz, k, b, jj) for b in bs for jj in range(2)]

        groupt = {}

        def transpose_features(g, c, dz, bs=(0, 1)):
            if (g, c) not in dzt:
                codes = dztp.tile([P, GT], U32, name="dzt_codes", tag="dztc", align_bytes=64)
                scales = dztp.tile([P, GT], U8, name="dzt_scales", tag="dzts", align_bytes=64)
                dzt[(g, c)] = (codes, scales)
            grouped = ilp.tile([P, HALF, J], BF16, name="groupedt", tag="il", align_bytes=64)
            groupt[(g, c)] = grouped
            gw = grouped[:].rearrange("p n t -> p (n t)").bitcast(F32)
            for b in bs:
                tp = ptp.tile([P, 2, 2, P], F32, name="tp", tag="tp")
                for jj in range(2):
                    words = dz[:, 2 * b + jj, :].bitcast(F32)
                    for u in range(2):
                        nc.tensor.transpose(tp[:, jj, u, :], words[:, u::2], ident[:])
                nc.scalar.copy(
                    out=gw[:, 512 * b : 512 * (b + 1)].rearrange("p (j r u) -> p j r u", j=2, u=2),
                    in_=tp[:].rearrange("p j u r -> p j r u"),
                )

        def quantise_columns(g, c, bs):
            codes, scales = dzt[(g, c)]
            cols = slice(256 * bs[0], 256 * (bs[-1] + 1))
            nc.vector.quantize_mx(
                out=codes[:, cols].bitcast(E5M2),
                scales=scales[:, cols],
                in_=groupt[(g, c)][:, cols, :].rearrange("p n t -> p (n t)"),
            )

        def quantise_features(g, c, bs=(0, 1)):
            return [partial(quantise_columns, g, c, bs)]

        uil = {}

        def token_rows(k, which, part):
            g, hf = UNITS[k]
            if part == 0:
                uil[(k, which)] = ilp.tile([P, HALF, J], BF16, name="il", tag="il", align_bytes=64)
            rows = uil[(k, which)][:].rearrange("p (h e) j -> p h e j", e=HD)
            if part == 0:
                c0 = 256 * which + 128 * hf
                src = udz0[g][:, :, c0 : c0 + 128].rearrange("p j (h f) -> p h f j", f=DK)
                nc.vector.tensor_copy(out=rows[:, :, 0:DK, :], in_=src)
            else:
                src = (udzg, udzv)[which][k][:].rearrange("p j (h f) -> p h f j", f=DV)
                nc.vector.tensor_copy(out=rows[:, :, DK:HD, :], in_=src)

        def token_quantise(k, which, lo, hi):
            g, hf = UNITS[k]
            if lo == 0:
                pool = keep if g == 0 else dzcp
                key = "%d%d" % (which, hf) if g == 0 else ""
                codes = pool.tile([P, HALF], U32, name="dzc" + key, align_bytes=64)
                scales = pool.tile([P, HALF], U8, name="dzs" + key, align_bytes=64)
                dzc[(g, which, hf)] = (codes, scales)
            codes, scales = dzc[(g, which, hf)]
            flat = uil[(k, which)][:].rearrange("p n j -> p (n j)")
            nc.vector.quantize_mx(
                out=codes[:, lo:hi].bitcast(E5M2), scales=scales[:, lo:hi], in_=flat[:, J * lo : J * hi]
            )

        def token_blocks(k, whichs=(0, 1)):
            steps = [partial(token_rows, k, which, part) for which in whichs for part in range(2)]
            return steps + [
                partial(token_quantise, k, which, lo, hi) for which in whichs for lo, hi in ((0, 512), (512, HALF))
            ]

        turn = [0]
        wide = [False, 0]

        def result_tile():
            wide[1] += 1
            if wide[0] and wide[1] % 2:
                return ld.tile([P, DIM], F32, name="res", tag="ld")
            return io.tile([P, DIM], F32, name="res", tag="io")

        def evacuate(out, acc, both):
            turn[0] += 1
            if both and turn[0] % 2:
                nc.vector.tensor_copy(out=out, in_=acc)
            else:
                nc.scalar.copy(out=out, in_=acc)

        def weight_rows(which, hf, m, both):
            dst = (out_1, out_2)[which]
            if True:
                res = result_tile()
                mc = slice(P * m, P * (m + 1))
                for n in range(2):
                    cols = slice(512 * n, 512 * (n + 1))
                    acc = pacc.tile([P, 512], F32, name="acc", tag="acc")
                    for g in range(2):
                        codes, scales = dzc[(g, which, hf)]
                        nc.tensor.matmul_mx(
                            out=acc[:],
                            lhsT=codes[:, mc].bitcast(E5M2),
                            lhsT_scale=scales[:, mc],
                            rhs=t_codes[g][:, cols].bitcast(E4M3),
                            rhs_scale=t_scales[g][:, cols],
                            start=(g == 0),
                            stop=(g == 1),
                        )
                    evacuate(res[:, cols], acc[:], both)
                r0 = HALF * hf + P * m
                nc.sync.dma_start(out=dst[r0 : r0 + P, :], in_=res[:])

        def weight_grad(which, hf, both=False):
            return [partial(weight_rows, which, hf, m, both) for m in range(HALF // P)]

        def token_passes(g, j, n, acc, passes, first, last):
            mc = slice(P * j, P * (j + 1))
            cols = slice(512 * n, 512 * (n + 1))
            for c in passes:
                codes, scales = dzt[(g, c)]
                nc.tensor.matmul_mx(
                    out=acc[:],
                    lhsT=codes[:, mc].bitcast(E5M2),
                    lhsT_scale=scales[:, mc],
                    rhs=w_codes[c][:, cols].bitcast(E4M3),
                    rhs_scale=w_scales[c][:, cols],
                    start=(c == first),
                    stop=(c == last),
                )

        opened = {}

        def open_tokens(g, js, passes):
            for j in js:
                for n in range(2):
                    first = None
                    if (g, j, n) not in opened:
                        opened[(g, j, n)] = pacc.tile([P, 512], F32, name="accx", tag="acc")
                        first = passes[0]
                    token_passes(g, j, n, opened[(g, j, n)], passes, first, None)

        def token_rows_grad(g, j, passes, both):
            rows = out_0[0, GT * g : GT * (g + 1), :].rearrange("(p j) w -> p j w", j=J)
            if True:
                res = result_tile()
                for n in range(2):
                    if (g, j, n) in opened:
                        acc = opened[(g, j, n)]
                        token_passes(g, j, n, acc, passes[-1:], None, passes[-1])
                    else:
                        acc = pacc.tile([P, 512], F32, name="accx", tag="acc")
                        token_passes(g, j, n, acc, passes, passes[0], passes[-1])
                    evacuate(res[:, 512 * n : 512 * (n + 1)], acc[:], both)
                nc.sync.dma_start(out=rows[:, j, :], in_=res[:])

        def token_grad(g, js, passes, both=False):
            return [partial(token_rows_grad, g, j, passes, both) for j in js]

        ua[0] = ld.tile([P, J, HALF], F32, name="saved", tag="ld")
        raw_t0 = ld.tile([P, J, DIM], BF16, name="raw_t0", tag="ld")
        load_slots(ua[0], qg, 0, 0, 0)
        load_token_columns(raw_t0, 0, 0)
        ud1[0] = load_grad(grad_1, 0, 0)
        load_token_columns(raw_t0, 0, 1)
        load_slots(ua[0], qg, 0, 0, 1)
        uc[0] = load_saved(kv, 0, 0)
        ud3[0] = load_grad(grad_3, 0, 0)
        load_rot()
        load_qk(0)
        load_unit(1)
        load_raw(*order[0])
        background = [partial(prepare, i, n) for i in range(len(order)) for n in range(2)]
        gate_scalar(0, 0)
        g0 = group_on_vector(raw_t0, 0)
        g1 = group_on_vector(raw_t0, 1)
        quantise_piece(g0, t_codes[0], t_scales[0], 0)
        quantise_piece(g1, t_codes[0], t_scales[0], 1)
        drain(gate_head(0, (0,)))
        gate_scalar(0, 1)
        spread_rot()
        cast_back(0)
        squares(0)
        drain(gate_tail(0, (0,)))
        v_products = products(0)
        drain([v_products.pop(0), v_products.pop(0)])
        drain(rotate_back(0))
        drain(v_products)

        def more(n=1):
            for _ in range(n):
                if background:
                    background.pop(0)()

        left = []
        for k in range(4):
            g, hf = UNITS[k]
            gates = (0, 1) if k else (1,)
            if k == 2:
                background = background + token_grad(0, [0, 1, 2, 3], [0, 1, 2, 3, 4])
            if k < 3:
                left = gate_head(k, gates) + [settle] + gate_tail(k, gates) + [settle] + left
                squares(k + 1)
                if hf == 0:
                    cast_back(k + 1)
                weave(factors(k), left)
                if k > 0 and k < 3:
                    more()
                transpose_features(g, 1 + hf, udzg[k])
                if k == 0:
                    corrections(k)
                gate_scalar(k + 1, 0)
                if k == 1:
                    more()
                if k > 0:
                    corrections(k)
                drain(left)
                settle()
                finish(k)
                settle()
                if hf == 1:
                    cast_back(k + 1)
                if k < 2:
                    load_unit(k + 2)
                more()
                gate_scalar(k + 1, 1)
                more()
                drain(rotate_back(k + 1))
                transpose_features(g, 3 + hf, udzv[k])
                if hf == 1:
                    transpose_features(g, 0, udz0[g])
                products_next = products(k + 1)
                for i in range(4):
                    products_next.pop(0)()
                drain(quantise_features(g, 1 + hf))
                settle()
                if k == 2:
                    drain(token_blocks(k, (0,)))
                drain(products_next)
                settle()
                more(2)
                left = quantise_features(g, 3 + hf)
                if hf == 1:
                    left = left + quantise_features(g, 0)
                left = left + token_blocks(k, (0, 1) if k < 2 else (1,))
            else:
                drain(background)
                background = weight_grad(0, 0) + weight_grad(1, 0)
                more(4)
                left = left + gate_head(3, (0,))
                weave(factors(k), left)
                drain(left)
                more(4)
                corrections(k)
                more(2)
                wide[0] = True
                open_tokens(1, [0, 1], [1, 3])
                finish(k)
                transpose_features(1, 4, udzv[3])
                transpose_features(1, 0, udz0[1])
                drain(token_blocks(3, (1,)))
                drain(quantise_features(1, 4))
                drain(quantise_features(1, 0))
                drain(gate_tail(3, (0,)))
                drain(gate_head(3, (1,)))
                last = weight_grad(1, 1, False)
                drain(last[0:3])
                transpose_features(1, 2, udzg[3], (0,))
                drain(last[3:5])
                drain(gate_tail(3, (1,)))
                drain(quantise_features(1, 2, (0,)))
                open_tokens(1, [0, 1], [0, 4])
                transpose_features(1, 2, udzg[3], (1,))
                drain(token_grad(1, [0, 1], [1, 3, 0, 4, 2], False))
                drain(token_blocks(3, (0,)))
                drain(quantise_features(1, 2, (1,)))
                drain(token_grad(1, [2, 3], [1, 3, 0, 4, 2], True))
                drain(weight_grad(0, 1, True))
